import numpy as np
import ml_dtypes


def mxq(x, axis, fmt="e4m3"):
    dtype, down = {"e4m3": (ml_dtypes.float8_e4m3fn, 7), "e5m2": (ml_dtypes.float8_e5m2, 14)}[fmt]
    v = np.moveaxis(np.asarray(x, np.float32).astype(ml_dtypes.bfloat16).astype(np.float64), axis, -1)
    blocks = v.reshape(v.shape[:-1] + (-1, 32))
    amax = np.abs(blocks).max(-1, keepdims=True)
    byte = np.maximum(np.where(amax > 0, np.frexp(amax)[1] - 1 + 127, 0) - down, 1)
    scale = np.exp2(byte - 127.0)
    codes = (blocks / scale).astype(np.float32).astype(dtype).astype(np.float64)
    return np.moveaxis((codes * scale).reshape(v.shape), -1, axis)


WIDE = False


def mx_kscale(k):
    if not WIDE:
        return np.ones(k)
    levels = np.array([10, -10, 5, -5, 0])
    a = np.random.permutation(np.resize(levels, k // 512 * 4)).reshape(k // 512, 4)
    idx = np.arange(k)
    return np.exp2(a[idx // 512, idx % 128 // 32])


BF16 = ml_dtypes.bfloat16


def bf(x):
    return np.asarray(x, np.float32).astype(BF16)


def f64(x):
    return np.asarray(x).astype(np.float64)


E2M1 = np.array([0.0, 0.5, 1.0, 1.5, 2.0, 3.0, 4.0, 6.0, -0.0, -0.5, -1.0, -1.5, -2.0, -3.0, -4.0, -6.0])


def pack_weight(w, fmt):
    k, n = w.shape
    w = f64(bf(w)).reshape(k // 32, 32, n)
    amax = np.abs(w).max(1)
    if fmt == "e4m3":
        byte = np.frexp(amax)[1] - 1 + 127 - 7
    else:
        mant, ex = np.frexp(amax / 6.0)
        byte = np.where(mant > 0.5, ex, ex - 1) + 127
    byte = np.clip(np.where(amax > 0, byte, 1), 1, 254)
    scaled = (w * np.exp2(127.0 - byte)[:, None, :]).reshape(k, n).astype(np.float32)
    by_word = np.ascontiguousarray(scaled.reshape(k // 512, 128, 4, n).transpose(0, 1, 3, 2))
    if fmt == "e4m3":
        words = by_word.astype(ml_dtypes.float8_e4m3fn).view(np.uint8)
    else:
        c = by_word.astype(ml_dtypes.float4_e2m1fn).view(np.uint8) & 0xF
        words = c[..., 0::2] | (c[..., 1::2] << 4)
    return np.ascontiguousarray(words), np.ascontiguousarray(byte.astype(np.uint8).reshape(k // 512, 16, n))


def unpack_weight(words, scales, fmt):
    g, p, n, _ = words.shape
    if fmt == "e4m3":
        vals = np.ascontiguousarray(words).view(ml_dtypes.float8_e4m3fn).astype(np.float64)
    else:
        nib = np.empty((g, p, n, 4), np.uint8)
        nib[..., 0::2] = words & 0xF
        nib[..., 1::2] = words >> 4
        vals = E2M1[nib]
    vals = vals * np.repeat(np.exp2(scales.astype(np.float64) - 127.0), 8, axis=1)[..., None]
    return vals.transpose(0, 1, 3, 2).reshape(g * 512, n)


B, I, H = 512, 1024, 1024
G = 3
QH = H % 2 ** 9 == 0


def sigmoid(v):
    return 1.0 / (1.0 + np.exp(-v))


def setup_inputs():
    s = mx_kscale(I)
    x = bf(np.random.standard_normal((B, I)) * s)
    hid = bf(np.random.standard_normal((B, H)))
    wx = np.random.standard_normal((G, I, H)) * 0.6 / np.sqrt(I) / s[None, :, None]
    wx_words, wx_scales = pack_weight(wx.reshape(-1, H), "e4m3")
    wh = bf(np.random.standard_normal((3, H, H)) * 0.6 / np.sqrt(H))
    bx = bf(np.random.standard_normal((3, H)) * 0.3)
    bh = bf(np.random.standard_normal((3, H)) * 0.3)
    return {"x": x,
            "hid": hid,
            "wx_words": wx_words,
            "wx_scales": wx_scales,
            "wh": wh,
            "bx": bx,
            "bh": bh}


def reference(x, hid, wx_words, wx_scales, wh, bx, bh):
    x, hid, wh, bx, bh = f64(x), f64(hid), f64(wh), f64(bx), f64(bh)
    px = mxq(x, 1, "e4m3") @ unpack_weight(wx_words, wx_scales, "e4m3").reshape(G, I, H)
    if QH:
        ph = mxq(hid, 1, "e4m3") @ mxq(wh, 1, "e4m3")
    else:
        ph = hid @ wh
    gx = px.transpose(1, 0, 2) + bx[None]
    gh = ph.transpose(1, 0, 2) + bh[None]
    r = sigmoid(gx[:, 0] + gh[:, 0])
    z = sigmoid(gx[:, 1] + gh[:, 1])
    n = np.tanh(gx[:, 2] + r * gh[:, 2])
    next_hid = (1.0 - z) * n + z * hid
    return next_hid

@@ -1,0 +1,229 @@
+from contextlib import ExitStack
+
+import concourse.mybir as mybir
+from concourse.masks import make_identity
+
+F32 = mybir.dt.float32
+BF16 = mybir.dt.bfloat16
+I32 = mybir.dt.int32
+U32 = mybir.dt.uint32
+U8 = mybir.dt.uint8
+FP8X4 = mybir.dt.float8_e4m3fn_x4
+ACT = mybir.ActivationFunctionType
+ALU = mybir.AluOpType
+
+P = 128
+PACK = 4
+K_PASS = P * PACK
+BATCH, K_DIM, FEATURES = 512, 1024, 1024
+PASSES = K_DIM // K_PASS
+ROW_SETS = BATCH // P
+GATE_R, GATE_Z, GATE_N = 0, 1, 2
+GATE_ORDER = (GATE_R, GATE_N, GATE_Z)
+
+COL_GROUPS = 2
+GROUP_COLS = FEATURES // COL_GROUPS
+GROUP_TILES = GROUP_COLS // P
+
+RUN = 4
+RUNS_ALL = GROUP_COLS // RUN
+VECTOR_RUNS = RUNS_ALL // 4
+
+FLOPS = 2 * BATCH * (K_DIM + K_DIM) * 3 * FEATURES
+
+
+def tile_grucellv2_e_kernel(tc, x, hid, wx_words, wx_scales, wh, bx, bh, out):
+    nc = tc.nc
+    stages = [(group, gate) for group in range(COL_GROUPS) for gate in GATE_ORDER]
+
+    with ExitStack() as ctx:
+        consts = ctx.enter_context(tc.tile_pool(name="consts", bufs=1))
+        resident = ctx.enter_context(tc.tile_pool(name="resident", bufs=1))
+        raw_pool = ctx.enter_context(tc.tile_pool(name="raw", bufs=len(stages) * PASSES))
+        grouped_pool = ctx.enter_context(tc.tile_pool(name="grouped", bufs=2 * PASSES))
+        wh_pool = ctx.enter_context(tc.tile_pool(name="wh_mx", bufs=3))
+        gate_pool = ctx.enter_context(tc.tile_pool(name="gates", bufs=3))
+        result_pool = ctx.enter_context(tc.tile_pool(name="result", bufs=3))
+        psum = ctx.enter_context(tc.psum_pool(name="psum", bufs=8))
+
+        x_rows = resident.tile([P, ROW_SETS, K_DIM], BF16)
+        nc.sync.dma_start(out=x_rows[:], in_=x.rearrange("(p a) k -> p a k", a=ROW_SETS))
+        hid_rows = resident.tile([P, ROW_SETS, K_DIM], BF16)
+        nc.sync.dma_start(out=hid_rows[:], in_=hid.rearrange("(p a) k -> p a k", a=ROW_SETS))
+
+        wx_planes = resident.tile([P, 3 * PASSES, FEATURES], U8, align_bytes=64)
+        nc.vector.memset(wx_planes[:].bitcast(I32), 0)
+        scale_rows = wx_scales.rearrange("g (quad r) n -> r quad g n", r=4)
+        for r in range(4):
+            nc.sync.dma_start(out=wx_planes[r:P:32, :, :].bitcast(I32), in_=scale_rows[r].bitcast(I32))
+
+        wx_codes = resident.tile([P, 3 * PASSES, FEATURES], U32, align_bytes=64)
+        wx_words_by_partition = wx_words.rearrange("g p n t -> p g (n t)").bitcast(I32)
+        wh_raw = {}
+        for s, (group, gate) in enumerate(stages):
+            cols = slice(group * GROUP_COLS, (group + 1) * GROUP_COLS)
+            both = slice(gate * PASSES, (gate + 1) * PASSES)
+            nc.sync.dma_start(out=wx_codes[:, both, cols].bitcast(I32), in_=wx_words_by_partition[:, both, cols])
+            for c in range(PASSES):
+                raw = raw_pool.tile([P, PACK, GROUP_COLS], BF16)
+                rows = wh[gate, c * K_PASS : (c + 1) * K_PASS, cols]
+                nc.sync.dma_start(out=raw[:], in_=rows.rearrange("(p t) n -> p t n", t=PACK))
+                wh_raw[(s, c)] = raw
+
+        identity = consts.tile([P, P], F32)
+        make_identity(nc, identity[:])
+
+        tiles_all = FEATURES // P
+        bias_rows = consts.tile([P, P], BF16)
+        nc.vector.memset(bias_rows[:], 0.0)
+        nc.scalar.dma_start(out=bias_rows[0 : 3 * tiles_all, :], in_=bx.rearrange("g (j p) -> (g j) p", p=P))
+        nc.scalar.dma_start(out=bias_rows[32 : 32 + 3 * tiles_all, :], in_=bh.rearrange("g (j p) -> (g j) p", p=P))
+        bias_rows_f32 = consts.tile([P, P], F32)
+        nc.vector.tensor_copy(out=bias_rows_f32[:], in_=bias_rows[:])
+        bias_bank = psum.tile([P, P], F32, tag="bank")
+        nc.tensor.transpose(bias_bank[:], bias_rows_f32[:], identity[:])
+        bias_cols = consts.tile([P, 64], F32)
+        nc.vector.tensor_copy(out=bias_cols[:], in_=bias_bank[:, 0:64])
+
+        def bias_of(first_row, gate):
+            return bias_cols[:, first_row + gate * tiles_all : first_row + (gate + 1) * tiles_all]
+
+        bias_r = consts.tile([P, tiles_all], F32)
+        nc.vector.tensor_tensor(out=bias_r[:], in0=bias_of(0, GATE_R), in1=bias_of(32, GATE_R), op=ALU.add)
+        minus_bias_z = consts.tile([P, tiles_all], F32)
+        nc.vector.scalar_tensor_tensor(
+            out=minus_bias_z[:], in0=bias_of(0, GATE_Z), scalar=-1.0, in1=bias_of(32, GATE_Z),
+            op0=ALU.mult, op1=ALU.subtract,
+        )
+        bias_xn = bias_of(0, GATE_N)
+        bias_hn = bias_of(32, GATE_N)
+
+        def quantise_rows(rows_tile, label):
+            words = rows_tile[:].bitcast(F32)
+            grouped = grouped_pool.tile([P, PASSES, BATCH * PACK], BF16, align_bytes=64, name="rows_grouped", bufs=2)
+            grouped_words = grouped[:].bitcast(F32).rearrange("p c (b u) -> p c b u", u=2)
+            half = K_PASS // 2
+            for a in range(ROW_SETS):
+                flipped = psum.tile([P, PASSES, 2, P], F32, tag="bank")
+                for c in range(PASSES):
+                    for u in range(2):
+                        nc.tensor.transpose(flipped[:, c, u, :], words[:, a, c * half + u : (c + 1) * half : 2], identity[:])
+                copy_out = nc.vector.tensor_copy if a % 2 == 0 else nc.scalar.copy
+                copy_out(out=grouped_words[:, :, a * P : (a + 1) * P, :], in_=flipped[:].rearrange("p c u b -> p c b u"))
+            codes = resident.tile([P, PASSES, BATCH], U32, align_bytes=64, name=label + "_codes")
+            scales = resident.tile([P, PASSES, BATCH], U8, align_bytes=64, name=label + "_scales")
+            for c in range(PASSES):
+                nc.vector.quantize_mx(out=codes[:, c, :].bitcast(FP8X4), scales=scales[:, c, :], in_=grouped[:, c, :])
+            return codes[:], scales[:]
+
+        x_mx = quantise_rows(x_rows, "x")
+        hid_mx = quantise_rows(hid_rows, "hid")
+
+        def quantise_wh(s):
+            codes = wh_pool.tile([P, PASSES, GROUP_COLS], U32, align_bytes=64, name="wh_codes")
+            scales = wh_pool.tile([P, PASSES, GROUP_COLS], U8, align_bytes=64, name="wh_scales")
+            grouped_tiles = []
+            for c in range(PASSES):
+                grouped = grouped_pool.tile([P, GROUP_COLS, PACK], BF16, align_bytes=64, name="wh_grouped")
+                src = wh_raw[(s, c)][:].rearrange("p t (n i) -> p n t i", i=RUN)
+                dst = grouped[:].rearrange("p (n i) t -> p n t i", i=RUN)
+                nc.vector.tensor_copy(out=dst[:, :VECTOR_RUNS], in_=src[:, :VECTOR_RUNS])
+                nc.scalar.copy(out=dst[:, VECTOR_RUNS:], in_=src[:, VECTOR_RUNS:])
+                grouped_tiles.append(grouped)
+            for c in range(PASSES):
+                nc.vector.quantize_mx(
+                    out=codes[:, c, :].bitcast(FP8X4), scales=scales[:, c, :],
+                    in_=grouped_tiles[c][:].rearrange("p n t -> p (n t)"),
+                )
+            return codes[:], scales[:]
+
+        def contract(bank, weights, rows_mx, j, start, stop):
+            w_codes, w_scales = weights
+            r_codes, r_scales = rows_mx
+            cols = slice(j * P, (j + 1) * P)
+            for c in range(PASSES):
+                nc.tensor.matmul_mx(
+                    out=bank[:],
+                    lhsT=w_codes[:, c, cols].bitcast(FP8X4), lhsT_scale=w_scales[:, c, cols],
+                    rhs=r_codes[:, c, :].bitcast(FP8X4), rhs_scale=r_scales[:, c, :],
+                    start=start and c == 0, stop=stop and c == PASSES - 1,
+                )
+
+        def multiply(s, wh_mx):
+            group, gate = stages[s]
+            cols = slice(group * GROUP_COLS, (group + 1) * GROUP_COLS)
+            both = slice(gate * PASSES, (gate + 1) * PASSES)
+            wx_mx = (wx_codes[:, both, cols], wx_planes[:, both, cols])
+            apart = gate == GATE_N
+            x_banks = [psum.tile([P, BATCH], F32, name="x_bank", tag="bank") for j in range(GROUP_TILES)]
+            for j in range(GROUP_TILES):
+                contract(x_banks[j], wx_mx, x_mx, j, start=True, stop=apart)
+            if not apart:
+                for j in range(GROUP_TILES):
+                    contract(x_banks[j], wh_mx, hid_mx, j, start=False, stop=True)
+                return x_banks, x_banks
+            hid_banks = [psum.tile([P, BATCH], F32, name="hid_bank", tag="bank") for j in range(GROUP_TILES)]
+            for j in range(GROUP_TILES):
+                contract(hid_banks[j], wh_mx, hid_mx, j, start=True, stop=True)
+            return x_banks, hid_banks
+
+        def gate_arithmetic(s, banks, r_gate):
+            group, gate = stages[s]
+            x_banks, hid_banks = banks
+            value = gate_pool.tile([P, GROUP_TILES, BATCH], F32, name="gate_value")
+            first = group * GROUP_TILES
+            if gate == GATE_R:
+                for j in range(GROUP_TILES):
+                    nc.scalar.activation(out=value[:, j, :], in_=x_banks[j][:], func=ACT.Sigmoid,
+                                         bias=bias_r[:, first + j : first + j + 1], scale=1.0)
+            elif gate == GATE_Z:
+                for j in range(GROUP_TILES):
+                    nc.scalar.activation(out=value[:, j, :], in_=x_banks[j][:], func=ACT.Sigmoid,
+                                         bias=minus_bias_z[:, first + j : first + j + 1], scale=-1.0)
+            else:
+                for j in range(GROUP_TILES):
+                    nc.vector.scalar_tensor_tensor(
+                        out=value[:, j, :], in0=hid_banks[j][:], scalar=bias_hn[:, first + j : first + j + 1],
+                        in1=r_gate[:, j, :], op0=ALU.add, op1=ALU.mult,
+                    )
+                for j in range(GROUP_TILES):
+                    nc.vector.tensor_tensor(out=value[:, j, :], in0=value[:, j, :], in1=x_banks[j][:], op=ALU.add)
+                    nc.scalar.activation(out=value[:, j, :], in_=value[:, j, :], func=ACT.Tanh,
+                                         bias=bias_xn[:, first + j : first + j + 1], scale=1.0)
+            return value
+
+        blend = resident.tile([P, ROW_SETS, FEATURES], F32)
+        out_rows = out.rearrange("(p a) h -> p a h", a=ROW_SETS)
+
+        def turn_back_and_blend(s, value):
+            group, gate = stages[s]
+            if gate == GATE_R:
+                return
+            flipped_banks = []
+            for j in range(GROUP_TILES):
+                flipped = psum.tile([P, ROW_SETS, P], F32, name="flipped_gate", tag="bank")
+                for a in range(ROW_SETS):
+                    nc.tensor.transpose(flipped[:, a, :], value[:, j, a * P : (a + 1) * P], identity[:])
+                flipped_banks.append(flipped)
+            tile_cols = [slice((group * GROUP_TILES + j) * P, (group * GROUP_TILES + j + 1) * P) for j in range(GROUP_TILES)]
+            if gate == GATE_N:
+                for j, cols in enumerate(tile_cols):
+                    nc.vector.tensor_tensor(out=blend[:, :, cols], in0=flipped_banks[j][:], in1=hid_rows[:, :, cols], op=ALU.subtract)
+                return
+            for j, cols in enumerate(tile_cols):
+                nc.vector.tensor_tensor(out=blend[:, :, cols], in0=blend[:, :, cols], in1=flipped_banks[j][:], op=ALU.mult)
+            for j, cols in enumerate(tile_cols):
+                result = result_pool.tile([P, ROW_SETS, P], F32)
+                nc.vector.tensor_tensor(out=result[:], in0=blend[:, :, cols], in1=hid_rows[:, :, cols], op=ALU.add)
+                nc.sync.dma_start(out=out_rows[:, :, cols], in_=result[:])
+
+        wh_mx = {0: quantise_wh(0)}
+        values = {}
+        for s in range(len(stages)):
+            if s + 1 < len(stages):
+                wh_mx[s + 1] = quantise_wh(s + 1)
+            banks = multiply(s, wh_mx[s])
+            if s > 0:
+                turn_back_and_blend(s - 1, values[s - 1])
+            values[s] = gate_arithmetic(s, banks, values.get(s - 1))
+        turn_back_and_blend(len(stages) - 1, values[len(stages) - 1])

@@ -27,7 +27,7 @@ GROUP_TILES = GROUP_COLS // P
 
 RUN = 4
 RUNS_ALL = GROUP_COLS // RUN
-VECTOR_RUNS = RUNS_ALL // 4
+VECTOR_RUNS = RUNS_ALL // 2
 
 FLOPS = 2 * BATCH * (K_DIM + K_DIM) * 3 * FEATURES
 
@@ -45,11 +45,18 @@ def tile_grucellv2_e_kernel(tc, x, hid, wx_words, wx_scales, wh, bx, bh, out):
         gate_pool = ctx.enter_context(tc.tile_pool(name="gates", bufs=3))
         result_pool = ctx.enter_context(tc.tile_pool(name="result", bufs=3))
         psum = ctx.enter_context(tc.psum_pool(name="psum", bufs=8))
+        ctx.enter_context(tc.manual_schedule())
+
+        warm = consts.tile([P, 2], F32)
+        nc.vector.memset(warm[:], 0.0)
+        nc.scalar.activation(out=warm[:, 1:2], in_=warm[:, 0:1], func=ACT.Sigmoid)
 
         x_rows = resident.tile([P, ROW_SETS, K_DIM], BF16)
-        nc.sync.dma_start(out=x_rows[:], in_=x.rearrange("(p a) k -> p a k", a=ROW_SETS))
         hid_rows = resident.tile([P, ROW_SETS, K_DIM], BF16)
-        nc.sync.dma_start(out=hid_rows[:], in_=hid.rearrange("(p a) k -> p a k", a=ROW_SETS))
+        for rows_tile, source in ((x_rows, x), (hid_rows, hid)):
+            by_partition = source.rearrange("(p a) k -> p a k", a=ROW_SETS)
+            for a in range(ROW_SETS):
+                nc.sync.dma_start(out=rows_tile[:, a, :], in_=by_partition[:, a, :])
 
         wx_planes = resident.tile([P, 3 * PASSES, FEATURES], U8, align_bytes=64)
         nc.vector.memset(wx_planes[:].bitcast(I32), 0)
@@ -63,40 +70,23 @@ def tile_grucellv2_e_kernel(tc, x, hid, wx_words, wx_scales, wh, bx, bh, out):
         for s, (group, gate) in enumerate(stages):
             cols = slice(group * GROUP_COLS, (group + 1) * GROUP_COLS)
             both = slice(gate * PASSES, (gate + 1) * PASSES)
-            nc.sync.dma_start(out=wx_codes[:, both, cols].bitcast(I32), in_=wx_words_by_partition[:, both, cols])
             for c in range(PASSES):
                 raw = raw_pool.tile([P, PACK, GROUP_COLS], BF16)
                 rows = wh[gate, c * K_PASS : (c + 1) * K_PASS, cols]
                 nc.sync.dma_start(out=raw[:], in_=rows.rearrange("(p t) n -> p t n", t=PACK))
                 wh_raw[(s, c)] = raw
+            nc.sync.dma_start(out=wx_codes[:, both, cols].bitcast(I32), in_=wx_words_by_partition[:, both, cols])
 
         identity = consts.tile([P, P], F32)
         make_identity(nc, identity[:])
+        identity_bf16 = consts.tile([P, P], BF16)
+        make_identity(nc, identity_bf16[:])
 
         tiles_all = FEATURES // P
         bias_rows = consts.tile([P, P], BF16)
         nc.vector.memset(bias_rows[:], 0.0)
         nc.scalar.dma_start(out=bias_rows[0 : 3 * tiles_all, :], in_=bx.rearrange("g (j p) -> (g j) p", p=P))
         nc.scalar.dma_start(out=bias_rows[32 : 32 + 3 * tiles_all, :], in_=bh.rearrange("g (j p) -> (g j) p", p=P))
-        bias_rows_f32 = consts.tile([P, P], F32)
-        nc.vector.tensor_copy(out=bias_rows_f32[:], in_=bias_rows[:])
-        bias_bank = psum.tile([P, P], F32, tag="bank")
-        nc.tensor.transpose(bias_bank[:], bias_rows_f32[:], identity[:])
-        bias_cols = consts.tile([P, 64], F32)
-        nc.vector.tensor_copy(out=bias_cols[:], in_=bias_bank[:, 0:64])
-
-        def bias_of(first_row, gate):
-            return bias_cols[:, first_row + gate * tiles_all : first_row + (gate + 1) * tiles_all]
-
-        bias_r = consts.tile([P, tiles_all], F32)
-        nc.vector.tensor_tensor(out=bias_r[:], in0=bias_of(0, GATE_R), in1=bias_of(32, GATE_R), op=ALU.add)
-        minus_bias_z = consts.tile([P, tiles_all], F32)
-        nc.vector.scalar_tensor_tensor(
-            out=minus_bias_z[:], in0=bias_of(0, GATE_Z), scalar=-1.0, in1=bias_of(32, GATE_Z),
-            op0=ALU.mult, op1=ALU.subtract,
-        )
-        bias_xn = bias_of(0, GATE_N)
-        bias_hn = bias_of(32, GATE_N)
 
         def quantise_rows(rows_tile, label):
             words = rows_tile[:].bitcast(F32)
@@ -118,6 +108,32 @@ def tile_grucellv2_e_kernel(tc, x, hid, wx_words, wx_scales, wh, bx, bh, out):
 
         x_mx = quantise_rows(x_rows, "x")
         hid_mx = quantise_rows(hid_rows, "hid")
+
+        hid_flipped = resident.tile([P, tiles_all, BATCH], BF16)
+        for j in range(tiles_all):
+            flipped_hid = psum.tile([P, ROW_SETS, P], BF16, tag="bank")
+            for a in range(ROW_SETS):
+                nc.tensor.transpose(flipped_hid[:, a, :], hid_rows[:, a, j * P : (j + 1) * P], identity_bf16[:])
+            copy_out = nc.vector.tensor_copy if j % 2 == 0 else nc.scalar.copy
+            copy_out(out=hid_flipped[:, j, :], in_=flipped_hid[:].rearrange("p a b -> p (a b)"))
+
+        bias_bank = psum.tile([P, P], BF16, tag="bank")
+        nc.tensor.transpose(bias_bank[:], bias_rows[:], identity_bf16[:])
+        bias_cols = consts.tile([P, 64], F32)
+        nc.vector.tensor_copy(out=bias_cols[:], in_=bias_bank[:, 0:64])
+
+        def bias_of(first_row, gate):
+            return bias_cols[:, first_row + gate * tiles_all : first_row + (gate + 1) * tiles_all]
+
+        bias_r = consts.tile([P, tiles_all], F32)
+        nc.vector.tensor_tensor(out=bias_r[:], in0=bias_of(0, GATE_R), in1=bias_of(32, GATE_R), op=ALU.add)
+        minus_bias_z = consts.tile([P, tiles_all], F32)
+        nc.vector.scalar_tensor_tensor(
+            out=minus_bias_z[:], in0=bias_of(0, GATE_Z), scalar=-1.0, in1=bias_of(32, GATE_Z),
+            op0=ALU.mult, op1=ALU.subtract,
+        )
+        bias_xn = bias_of(0, GATE_N)
+        bias_hn = bias_of(32, GATE_N)
 
         def quantise_wh(s):
             codes = wh_pool.tile([P, PASSES, GROUP_COLS], U32, align_bytes=64, name="wh_codes")
@@ -154,20 +170,22 @@ def tile_grucellv2_e_kernel(tc, x, hid, wx_words, wx_scales, wh, bx, bh, out):
             cols = slice(group * GROUP_COLS, (group + 1) * GROUP_COLS)
             both = slice(gate * PASSES, (gate + 1) * PASSES)
             wx_mx = (wx_codes[:, both, cols], wx_planes[:, both, cols])
-            apart = gate == GATE_N
-            x_banks = [psum.tile([P, BATCH], F32, name="x_bank", tag="bank") for j in range(GROUP_TILES)]
-            for j in range(GROUP_TILES):
-                contract(x_banks[j], wx_mx, x_mx, j, start=True, stop=apart)
-            if not apart:
+            if gate == GATE_N:
+                hid_banks = [psum.tile([P, BATCH], F32, name="hid_bank", tag="bank") for j in range(GROUP_TILES)]
                 for j in range(GROUP_TILES):
-                    contract(x_banks[j], wh_mx, hid_mx, j, start=False, stop=True)
-                return x_banks, x_banks
-            hid_banks = [psum.tile([P, BATCH], F32, name="hid_bank", tag="bank") for j in range(GROUP_TILES)]
+                    contract(hid_banks[j], wh_mx, hid_mx, j, start=True, stop=True)
+                x_banks = [psum.tile([P, BATCH], F32, name="x_bank", tag="bank") for j in range(GROUP_TILES)]
+                for j in range(GROUP_TILES):
+                    contract(x_banks[j], wx_mx, x_mx, j, start=True, stop=True)
+                return x_banks, hid_banks
+            sum_banks = [psum.tile([P, BATCH], F32, name="sum_bank", tag="bank") for j in range(GROUP_TILES)]
             for j in range(GROUP_TILES):
-                contract(hid_banks[j], wh_mx, hid_mx, j, start=True, stop=True)
-            return x_banks, hid_banks
+                contract(sum_banks[j], wx_mx, x_mx, j, start=True, stop=False)
+            for j in range(GROUP_TILES):
+                contract(sum_banks[j], wh_mx, hid_mx, j, start=False, stop=True)
+            return sum_banks, sum_banks
 
-        def gate_arithmetic(s, banks, r_gate):
+        def gate_arithmetic(s, banks, before):
             group, gate = stages[s]
             x_banks, hid_banks = banks
             value = gate_pool.tile([P, GROUP_TILES, BATCH], F32, name="gate_value")
@@ -180,41 +198,39 @@ def tile_grucellv2_e_kernel(tc, x, hid, wx_words, wx_scales, wh, bx, bh, out):
                 for j in range(GROUP_TILES):
                     nc.scalar.activation(out=value[:, j, :], in_=x_banks[j][:], func=ACT.Sigmoid,
                                          bias=minus_bias_z[:, first + j : first + j + 1], scale=-1.0)
+                    nc.vector.tensor_tensor(out=value[:, j, :], in0=value[:, j, :], in1=before[:, j, :], op=ALU.mult)
             else:
-                for j in range(GROUP_TILES):
-                    nc.vector.scalar_tensor_tensor(
-                        out=value[:, j, :], in0=hid_banks[j][:], scalar=bias_hn[:, first + j : first + j + 1],
-                        in1=r_gate[:, j, :], op0=ALU.add, op1=ALU.mult,
-                    )
-                for j in range(GROUP_TILES):
-                    nc.vector.tensor_tensor(out=value[:, j, :], in0=value[:, j, :], in1=x_banks[j][:], op=ALU.add)
-                    nc.scalar.activation(out=value[:, j, :], in_=value[:, j, :], func=ACT.Tanh,
-                                         bias=bias_xn[:, first + j : first + j + 1], scale=1.0)
+                for j in range(GROUP_TILES + 1):
+                    if j < GROUP_TILES:
+                        nc.vector.scalar_tensor_tensor(
+                            out=value[:, j, :], in0=hid_banks[j][:], scalar=bias_hn[:, first + j : first + j + 1],
+                            in1=before[:, j, :], op0=ALU.add, op1=ALU.mult,
+                        )
+                    if j > 0:
+                        i = j - 1
+                        nc.vector.tensor_tensor(out=value[:, i, :], in0=value[:, i, :], in1=x_banks[i][:], op=ALU.add)
+                        nc.scalar.activation(out=value[:, i, :], in_=value[:, i, :], func=ACT.Tanh,
+                                             bias=bias_xn[:, first + i : first + i + 1], scale=1.0)
+                        nc.gpsimd.tensor_tensor(out=value[:, i, :], in0=value[:, i, :],
+                                                in1=hid_flipped[:, first + i, :], op=ALU.subtract)
             return value
 
-        blend = resident.tile([P, ROW_SETS, FEATURES], F32)
         out_rows = out.rearrange("(p a) h -> p a h", a=ROW_SETS)
 
-        def turn_back_and_blend(s, value):
+        def turn_back_and_store(s, value):
             group, gate = stages[s]
-            if gate == GATE_R:
+            if gate != GATE_ORDER[-1]:
                 return
             flipped_banks = []
             for j in range(GROUP_TILES):
-                flipped = psum.tile([P, ROW_SETS, P], F32, name="flipped_gate", tag="bank")
+                flipped = psum.tile([P, ROW_SETS, P], F32, name="flipped_product", tag="bank")
                 for a in range(ROW_SETS):
                     nc.tensor.transpose(flipped[:, a, :], value[:, j, a * P : (a + 1) * P], identity[:])
                 flipped_banks.append(flipped)
-            tile_cols = [slice((group * GROUP_TILES + j) * P, (group * GROUP_TILES + j + 1) * P) for j in range(GROUP_TILES)]
-            if gate == GATE_N:
-                for j, cols in enumerate(tile_cols):
-                    nc.vector.tensor_tensor(out=blend[:, :, cols], in0=flipped_banks[j][:], in1=hid_rows[:, :, cols], op=ALU.subtract)
-                return
-            for j, cols in enumerate(tile_cols):
-                nc.vector.tensor_tensor(out=blend[:, :, cols], in0=blend[:, :, cols], in1=flipped_banks[j][:], op=ALU.mult)
-            for j, cols in enumerate(tile_cols):
+            for j in range(GROUP_TILES):
+                cols = slice((group * GROUP_TILES + j) * P, (group * GROUP_TILES + j + 1) * P)
                 result = result_pool.tile([P, ROW_SETS, P], F32)
-                nc.vector.tensor_tensor(out=result[:], in0=blend[:, :, cols], in1=hid_rows[:, :, cols], op=ALU.add)
+                nc.vector.tensor_tensor(out=result[:], in0=flipped_banks[j][:], in1=hid_rows[:, :, cols], op=ALU.add)
                 nc.sync.dma_start(out=out_rows[:, :, cols], in_=result[:])
 
         wh_mx = {0: quantise_wh(0)}
@@ -224,6 +240,6 @@ def tile_grucellv2_e_kernel(tc, x, hid, wx_words, wx_scales, wh, bx, bh, out):
                 wh_mx[s + 1] = quantise_wh(s + 1)
             banks = multiply(s, wh_mx[s])
             if s > 0:
-                turn_back_and_blend(s - 1, values[s - 1])
+                turn_back_and_store(s - 1, values[s - 1])
             values[s] = gate_arithmetic(s, banks, values.get(s - 1))
-        turn_back_and_blend(len(stages) - 1, values[len(stages) - 1])
+        turn_back_and_store(len(stages) - 1, values[len(stages) - 1])

@@ -45,7 +45,6 @@ def tile_grucellv2_e_kernel(tc, x, hid, wx_words, wx_scales, wh, bx, bh, out):
         gate_pool = ctx.enter_context(tc.tile_pool(name="gates", bufs=3))
         result_pool = ctx.enter_context(tc.tile_pool(name="result", bufs=3))
         psum = ctx.enter_context(tc.psum_pool(name="psum", bufs=8))
-        ctx.enter_context(tc.manual_schedule())
 
         warm = consts.tile([P, 2], F32)
         nc.vector.memset(warm[:], 0.0)

@@ -19,77 +19,101 @@ BATCH, K_DIM, FEATURES = 512, 1024, 1024
 PASSES = K_DIM // K_PASS
 ROW_SETS = BATCH // P
 GATE_R, GATE_Z, GATE_N = 0, 1, 2
-GATE_ORDER = (GATE_R, GATE_N, GATE_Z)
 
-COL_GROUPS = 2
-GROUP_COLS = FEATURES // COL_GROUPS
+GROUPS = 2
+GROUP_COLS = FEATURES // GROUPS
 GROUP_TILES = GROUP_COLS // P
+TILES = FEATURES // P
 
 RUN = 4
 RUNS_ALL = GROUP_COLS // RUN
-VECTOR_RUNS = RUNS_ALL // 2
+VECTOR_SHARE = {(0, 0): 64, (2, 0): 64, (1, 0): 64, (0, 1): 64, (2, 1): 128, (1, 1): 64}
 
 FLOPS = 2 * BATCH * (K_DIM + K_DIM) * 3 * FEATURES
 
 
 def tile_grucellv2_e_kernel(tc, x, hid, wx_words, wx_scales, wh, bx, bh, out):
     nc = tc.nc
-    stages = [(group, gate) for group in range(COL_GROUPS) for gate in GATE_ORDER]
 
     with ExitStack() as ctx:
         consts = ctx.enter_context(tc.tile_pool(name="consts", bufs=1))
         resident = ctx.enter_context(tc.tile_pool(name="resident", bufs=1))
-        raw_pool = ctx.enter_context(tc.tile_pool(name="raw", bufs=len(stages) * PASSES))
-        grouped_pool = ctx.enter_context(tc.tile_pool(name="grouped", bufs=2 * PASSES))
-        wh_pool = ctx.enter_context(tc.tile_pool(name="wh_mx", bufs=3))
-        gate_pool = ctx.enter_context(tc.tile_pool(name="gates", bufs=3))
-        result_pool = ctx.enter_context(tc.tile_pool(name="result", bufs=3))
+        raw_pool = ctx.enter_context(tc.tile_pool(name="raw", bufs=3 * PASSES * GROUPS))
+        grouped_pool = ctx.enter_context(tc.tile_pool(name="grouped", bufs=4))
+        gate_pool = ctx.enter_context(tc.tile_pool(name="gates", bufs=GROUP_TILES))
+        result_pool = ctx.enter_context(tc.tile_pool(name="result", bufs=4))
         psum = ctx.enter_context(tc.psum_pool(name="psum", bufs=8))
+        ctx.enter_context(tc.manual_schedule())
 
         warm = consts.tile([P, 2], F32)
         nc.vector.memset(warm[:], 0.0)
         nc.scalar.activation(out=warm[:, 1:2], in_=warm[:, 0:1], func=ACT.Sigmoid)
 
+        bias_rows = consts.tile([P, P], BF16)
+        nc.vector.memset(bias_rows[:], 0.0)
+        nc.scalar.dma_start(out=bias_rows[0 : 3 * TILES, :], in_=bx.rearrange("g (j p) -> (g j) p", p=P))
+        nc.scalar.dma_start(out=bias_rows[32 : 32 + 3 * TILES, :], in_=bh.rearrange("g (j p) -> (g j) p", p=P))
+
         x_rows = resident.tile([P, ROW_SETS, K_DIM], BF16)
         hid_rows = resident.tile([P, ROW_SETS, K_DIM], BF16)
-        for rows_tile, source in ((x_rows, x), (hid_rows, hid)):
+
+        def load_rows(rows_tile, source):
             by_partition = source.rearrange("(p a) k -> p a k", a=ROW_SETS)
             for a in range(ROW_SETS):
                 nc.sync.dma_start(out=rows_tile[:, a, :], in_=by_partition[:, a, :])
 
         wx_planes = resident.tile([P, 3 * PASSES, FEATURES], U8, align_bytes=64)
-        nc.vector.memset(wx_planes[:].bitcast(I32), 0)
         scale_rows = wx_scales.rearrange("g (quad r) n -> r quad g n", r=4)
-        for r in range(4):
-            nc.sync.dma_start(out=wx_planes[r:P:32, :, :].bitcast(I32), in_=scale_rows[r].bitcast(I32))
+
+        def load_planes(planes):
+            for r in range(4):
+                nc.sync.dma_start(out=wx_planes[r:P:32, planes, :].bitcast(I32), in_=scale_rows[r][:, planes, :].bitcast(I32))
+
+        first_planes = slice(0, PASSES)
+        later_planes = slice(PASSES, 3 * PASSES)
+        nc.vector.memset(wx_planes[:, first_planes, :].bitcast(I32), 0)
+        nc.vector.memset(wx_planes[:, later_planes, :].bitcast(I32), 0)
 
         wx_codes = resident.tile([P, 3 * PASSES, FEATURES], U32, align_bytes=64)
         wx_words_by_partition = wx_words.rearrange("g p n t -> p g (n t)").bitcast(I32)
-        wh_raw = {}
-        for s, (group, gate) in enumerate(stages):
+
+        def load_wx(gate, group):
             cols = slice(group * GROUP_COLS, (group + 1) * GROUP_COLS)
             both = slice(gate * PASSES, (gate + 1) * PASSES)
+            nc.sync.dma_start(out=wx_codes[:, both, cols].bitcast(I32), in_=wx_words_by_partition[:, both, cols])
+
+        wh_raw = {}
+
+        def load_wh(gate, group):
+            cols = slice(group * GROUP_COLS, (group + 1) * GROUP_COLS)
             for c in range(PASSES):
                 raw = raw_pool.tile([P, PACK, GROUP_COLS], BF16)
                 rows = wh[gate, c * K_PASS : (c + 1) * K_PASS, cols]
                 nc.sync.dma_start(out=raw[:], in_=rows.rearrange("(p t) n -> p t n", t=PACK))
-                wh_raw[(s, c)] = raw
-            nc.sync.dma_start(out=wx_codes[:, both, cols].bitcast(I32), in_=wx_words_by_partition[:, both, cols])
+                wh_raw[(gate, c, group)] = raw
+
+        load_rows(hid_rows, hid)
+        load_rows(x_rows, x)
+        load_wh(GATE_R, 0)
+        load_planes(first_planes)
+        load_wx(GATE_R, 0)
+        load_wh(GATE_N, 0)
+        load_planes(later_planes)
+        load_wx(GATE_N, 0)
+        load_wh(GATE_Z, 0)
+        load_wx(GATE_Z, 0)
+        for gate in (GATE_R, GATE_N, GATE_Z):
+            load_wh(gate, 1)
+            load_wx(gate, 1)
 
         identity = consts.tile([P, P], F32)
         make_identity(nc, identity[:])
         identity_bf16 = consts.tile([P, P], BF16)
         make_identity(nc, identity_bf16[:])
 
-        tiles_all = FEATURES // P
-        bias_rows = consts.tile([P, P], BF16)
-        nc.vector.memset(bias_rows[:], 0.0)
-        nc.scalar.dma_start(out=bias_rows[0 : 3 * tiles_all, :], in_=bx.rearrange("g (j p) -> (g j) p", p=P))
-        nc.scalar.dma_start(out=bias_rows[32 : 32 + 3 * tiles_all, :], in_=bh.rearrange("g (j p) -> (g j) p", p=P))
-
-        def quantise_rows(rows_tile, label):
+        def flip_rows(rows_tile, label):
             words = rows_tile[:].bitcast(F32)
-            grouped = grouped_pool.tile([P, PASSES, BATCH * PACK], BF16, align_bytes=64, name="rows_grouped", bufs=2)
+            grouped = resident.tile([P, PASSES, BATCH * PACK], BF16, align_bytes=64, name=label + "_grouped")
             grouped_words = grouped[:].bitcast(F32).rearrange("p c (b u) -> p c b u", u=2)
             half = K_PASS // 2
             for a in range(ROW_SETS):
@@ -97,148 +121,210 @@ def tile_grucellv2_e_kernel(tc, x, hid, wx_words, wx_scales, wh, bx, bh, out):
                 for c in range(PASSES):
                     for u in range(2):
                         nc.tensor.transpose(flipped[:, c, u, :], words[:, a, c * half + u : (c + 1) * half : 2], identity[:])
-                copy_out = nc.vector.tensor_copy if a % 2 == 0 else nc.scalar.copy
+                copy_out = nc.vector.tensor_copy if a % 2 == 1 else nc.scalar.copy
                 copy_out(out=grouped_words[:, :, a * P : (a + 1) * P, :], in_=flipped[:].rearrange("p c u b -> p c b u"))
+            return grouped
+
+        def quantise_rows(grouped, label):
             codes = resident.tile([P, PASSES, BATCH], U32, align_bytes=64, name=label + "_codes")
             scales = resident.tile([P, PASSES, BATCH], U8, align_bytes=64, name=label + "_scales")
             for c in range(PASSES):
                 nc.vector.quantize_mx(out=codes[:, c, :].bitcast(FP8X4), scales=scales[:, c, :], in_=grouped[:, c, :])
             return codes[:], scales[:]
 
-        x_mx = quantise_rows(x_rows, "x")
-        hid_mx = quantise_rows(hid_rows, "hid")
+        wh_codes, wh_scales, wh_grouped = {}, {}, {}
 
-        hid_flipped = resident.tile([P, tiles_all, BATCH], BF16)
-        for j in range(tiles_all):
-            flipped_hid = psum.tile([P, ROW_SETS, P], BF16, tag="bank")
+        def regroup(gate, c, group):
+            grouped = grouped_pool.tile([P, GROUP_COLS, PACK], BF16, align_bytes=64)
+            src = wh_raw[(gate, c, group)][:].rearrange("p t (n i) -> p n t i", i=RUN)
+            dst = grouped[:].rearrange("p (n i) t -> p n t i", i=RUN)
+            runs = VECTOR_SHARE[(gate, group)]
+            if runs > 0:
+                nc.vector.tensor_copy(out=dst[:, :runs], in_=src[:, :runs])
+            if runs < RUNS_ALL:
+                nc.scalar.copy(out=dst[:, runs:], in_=src[:, runs:])
+            wh_grouped[(gate, c, group)] = grouped
+
+        def quantise(gate, c, group):
+            codes = resident.tile([P, GROUP_COLS], U32, align_bytes=64, name="wh_codes_%d_%d_%d" % (gate, c, group))
+            scales = resident.tile([P, GROUP_COLS], U8, align_bytes=64, name="wh_scales_%d_%d_%d" % (gate, c, group))
+            nc.vector.quantize_mx(
+                out=codes[:].bitcast(FP8X4), scales=scales[:],
+                in_=wh_grouped[(gate, c, group)][:].rearrange("p n t -> p (n t)"),
+            )
+            wh_codes[(gate, c, group)] = codes
+            wh_scales[(gate, c, group)] = scales
+
+        def prepare(gate, group):
+            for c in range(PASSES):
+                regroup(gate, c, group)
+            for c in range(PASSES):
+                quantise(gate, c, group)
+
+        def new_bank():
+            return psum.tile([P, BATCH], F32, name="bank", tag="bank")
+
+        def x_pass(bank, gate, j, c, start, stop):
+            cols = slice(j * P, (j + 1) * P)
+            g = gate * PASSES + c
+            nc.tensor.matmul_mx(
+                out=bank[:], lhsT=wx_codes[:, g, cols].bitcast(FP8X4), lhsT_scale=wx_planes[:, g, cols],
+                rhs=x_codes[:, c, :].bitcast(FP8X4), rhs_scale=x_scales[:, c, :], start=start, stop=stop,
+            )
+
+        def hid_pass(bank, gate, j, c, start, stop):
+            group, i = divmod(j, GROUP_TILES)
+            cols = slice(i * P, (i + 1) * P)
+            nc.tensor.matmul_mx(
+                out=bank[:],
+                lhsT=wh_codes[(gate, c, group)][:, cols].bitcast(FP8X4), lhsT_scale=wh_scales[(gate, c, group)][:, cols],
+                rhs=hid_codes[:, c, :].bitcast(FP8X4), rhs_scale=hid_scales[:, c, :], start=start, stop=stop,
+            )
+
+        def tiles_of(group):
+            return range(group * GROUP_TILES, (group + 1) * GROUP_TILES)
+
+        r_value, y_value, n_value, z_value = {}, {}, {}, {}
+        r_bank, nh_bank, nx_bank, z_bank, y_flipped, z_flipped = {}, {}, {}, {}, {}, {}
+
+        def sigmoid_r(j):
+            r_value[j] = gate_pool.tile([P, BATCH], F32, name="r_value")
+            nc.scalar.activation(out=r_value[j][:], in_=r_bank[j][:], func=ACT.Sigmoid, bias=bias_r[:, j : j + 1], scale=1.0)
+
+        def step_t(j):
+            y_value[j] = gate_pool.tile([P, BATCH], F32, name="y_value")
+            nc.vector.scalar_tensor_tensor(
+                out=y_value[j][:], in0=nh_bank[j][:], scalar=bias_hn[:, j : j + 1], in1=r_value[j][:], op0=ALU.add, op1=ALU.mult,
+            )
+
+        def step_y(j):
+            nc.vector.scalar_tensor_tensor(
+                out=y_value[j][:], in0=nx_bank[j][:], scalar=bias_xn[:, j : j + 1], in1=y_value[j][:], op0=ALU.add, op1=ALU.add,
+            )
+
+        def flip(value, name):
+            flipped = psum.tile([P, ROW_SETS, P], F32, name=name, tag="bank")
             for a in range(ROW_SETS):
-                nc.tensor.transpose(flipped_hid[:, a, :], hid_rows[:, a, j * P : (j + 1) * P], identity_bf16[:])
-            copy_out = nc.vector.tensor_copy if j % 2 == 0 else nc.scalar.copy
-            copy_out(out=hid_flipped[:, j, :], in_=flipped_hid[:].rearrange("p a b -> p (a b)"))
+                nc.tensor.transpose(flipped[:, a, :], value[:, a * P : (a + 1) * P], identity[:])
+            return flipped
 
+        def flip_y(j):
+            y_flipped[j] = flip(y_value[j], "y_flipped")
+
+        def flip_z(j):
+            z_flipped[j] = flip(z_value[j], "z_flipped")
+
+        def tanh_n(j):
+            n_value[j] = gate_pool.tile([P, ROW_SETS, P], F32, name="n_value")
+            nc.scalar.activation(out=n_value[j][:], in_=y_flipped[j][:], func=ACT.Tanh)
+
+        def step_d(j):
+            engine = nc.gpsimd
+            engine.tensor_tensor(out=n_value[j][:], in0=n_value[j][:], in1=hid_rows[:, :, j * P : (j + 1) * P], op=ALU.subtract)
+
+        def sigmoid_z(j):
+            z_value[j] = gate_pool.tile([P, BATCH], F32, name="z_value", bufs=GROUP_TILES)
+            nc.scalar.activation(out=z_value[j][:], in_=z_bank[j][:], func=ACT.Sigmoid, bias=minus_bias_z[:, j : j + 1], scale=-1.0)
+
+        out_rows = out.rearrange("(p a) h -> p a h", a=ROW_SETS)
+        results = {}
+
+        def step_e(j):
+            results[j] = result_pool.tile([P, ROW_SETS, P], F32, name="result")
+            nc.vector.tensor_tensor(out=results[j][:], in0=z_flipped[j][:], in1=n_value[j][:], op=ALU.mult)
+
+        def finish(j):
+            cols = slice(j * P, (j + 1) * P)
+            engine = nc.vector
+            engine.tensor_tensor(out=results[j][:], in0=results[j][:], in1=hid_rows[:, :, cols], op=ALU.add)
+            nc.sync.dma_start(out=out_rows[:, :, cols], in_=results[j][:])
+
+        def x_half(banks, gate, group, start, stop):
+            for j in tiles_of(group):
+                if start:
+                    banks[j] = new_bank()
+                for c in range(PASSES):
+                    x_pass(banks[j], gate, j, c, start and c == 0, stop and c == PASSES - 1)
+
+        def hid_half(banks, gate, group, start, stop):
+            for j in tiles_of(group):
+                if start:
+                    banks[j] = new_bank()
+                for c in range(PASSES):
+                    hid_pass(banks[j], gate, j, c, start and c == 0, stop and c == PASSES - 1)
+
+        hid_grouped = flip_rows(hid_rows, "hid")
+        hid_codes, hid_scales = quantise_rows(hid_grouped, "hid")
+        prepare(GATE_R, 0)
+        x_grouped = flip_rows(x_rows, "x")
+        x_codes, x_scales = quantise_rows(x_grouped, "x")
         bias_bank = psum.tile([P, P], BF16, tag="bank")
         nc.tensor.transpose(bias_bank[:], bias_rows[:], identity_bf16[:])
         bias_cols = consts.tile([P, 64], F32)
         nc.vector.tensor_copy(out=bias_cols[:], in_=bias_bank[:, 0:64])
 
         def bias_of(first_row, gate):
-            return bias_cols[:, first_row + gate * tiles_all : first_row + (gate + 1) * tiles_all]
+            return bias_cols[:, first_row + gate * TILES : first_row + (gate + 1) * TILES]
 
-        bias_r = consts.tile([P, tiles_all], F32)
+        bias_r = consts.tile([P, TILES], F32)
         nc.vector.tensor_tensor(out=bias_r[:], in0=bias_of(0, GATE_R), in1=bias_of(32, GATE_R), op=ALU.add)
-        minus_bias_z = consts.tile([P, tiles_all], F32)
+        minus_bias_z = consts.tile([P, TILES], F32)
         nc.vector.scalar_tensor_tensor(
-            out=minus_bias_z[:], in0=bias_of(0, GATE_Z), scalar=-1.0, in1=bias_of(32, GATE_Z),
-            op0=ALU.mult, op1=ALU.subtract,
+            out=minus_bias_z[:], in0=bias_of(0, GATE_Z), scalar=-1.0, in1=bias_of(32, GATE_Z), op0=ALU.mult, op1=ALU.subtract,
         )
         bias_xn = bias_of(0, GATE_N)
         bias_hn = bias_of(32, GATE_N)
 
-        def quantise_wh(s):
-            codes = wh_pool.tile([P, PASSES, GROUP_COLS], U32, align_bytes=64, name="wh_codes")
-            scales = wh_pool.tile([P, PASSES, GROUP_COLS], U8, align_bytes=64, name="wh_scales")
-            grouped_tiles = []
-            for c in range(PASSES):
-                grouped = grouped_pool.tile([P, GROUP_COLS, PACK], BF16, align_bytes=64, name="wh_grouped")
-                src = wh_raw[(s, c)][:].rearrange("p t (n i) -> p n t i", i=RUN)
-                dst = grouped[:].rearrange("p (n i) t -> p n t i", i=RUN)
-                nc.vector.tensor_copy(out=dst[:, :VECTOR_RUNS], in_=src[:, :VECTOR_RUNS])
-                nc.scalar.copy(out=dst[:, VECTOR_RUNS:], in_=src[:, VECTOR_RUNS:])
-                grouped_tiles.append(grouped)
-            for c in range(PASSES):
-                nc.vector.quantize_mx(
-                    out=codes[:, c, :].bitcast(FP8X4), scales=scales[:, c, :],
-                    in_=grouped_tiles[c][:].rearrange("p n t -> p (n t)"),
-                )
-            return codes[:], scales[:]
-
-        def contract(bank, weights, rows_mx, j, start, stop):
-            w_codes, w_scales = weights
-            r_codes, r_scales = rows_mx
-            cols = slice(j * P, (j + 1) * P)
-            for c in range(PASSES):
-                nc.tensor.matmul_mx(
-                    out=bank[:],
-                    lhsT=w_codes[:, c, cols].bitcast(FP8X4), lhsT_scale=w_scales[:, c, cols],
-                    rhs=r_codes[:, c, :].bitcast(FP8X4), rhs_scale=r_scales[:, c, :],
-                    start=start and c == 0, stop=stop and c == PASSES - 1,
-                )
-
-        def multiply(s, wh_mx):
-            group, gate = stages[s]
-            cols = slice(group * GROUP_COLS, (group + 1) * GROUP_COLS)
-            both = slice(gate * PASSES, (gate + 1) * PASSES)
-            wx_mx = (wx_codes[:, both, cols], wx_planes[:, both, cols])
-            if gate == GATE_N:
-                hid_banks = [psum.tile([P, BATCH], F32, name="hid_bank", tag="bank") for j in range(GROUP_TILES)]
-                for j in range(GROUP_TILES):
-                    contract(hid_banks[j], wh_mx, hid_mx, j, start=True, stop=True)
-                x_banks = [psum.tile([P, BATCH], F32, name="x_bank", tag="bank") for j in range(GROUP_TILES)]
-                for j in range(GROUP_TILES):
-                    contract(x_banks[j], wx_mx, x_mx, j, start=True, stop=True)
-                return x_banks, hid_banks
-            sum_banks = [psum.tile([P, BATCH], F32, name="sum_bank", tag="bank") for j in range(GROUP_TILES)]
-            for j in range(GROUP_TILES):
-                contract(sum_banks[j], wx_mx, x_mx, j, start=True, stop=False)
-            for j in range(GROUP_TILES):
-                contract(sum_banks[j], wh_mx, hid_mx, j, start=False, stop=True)
-            return sum_banks, sum_banks
-
-        def gate_arithmetic(s, banks, before):
-            group, gate = stages[s]
-            x_banks, hid_banks = banks
-            value = gate_pool.tile([P, GROUP_TILES, BATCH], F32, name="gate_value")
-            first = group * GROUP_TILES
-            if gate == GATE_R:
-                for j in range(GROUP_TILES):
-                    nc.scalar.activation(out=value[:, j, :], in_=x_banks[j][:], func=ACT.Sigmoid,
-                                         bias=bias_r[:, first + j : first + j + 1], scale=1.0)
-            elif gate == GATE_Z:
-                for j in range(GROUP_TILES):
-                    nc.scalar.activation(out=value[:, j, :], in_=x_banks[j][:], func=ACT.Sigmoid,
-                                         bias=minus_bias_z[:, first + j : first + j + 1], scale=-1.0)
-                    nc.vector.tensor_tensor(out=value[:, j, :], in0=value[:, j, :], in1=before[:, j, :], op=ALU.mult)
+        for group in range(GROUPS):
+            if group == 0:
+                hid_half(r_bank, GATE_R, group, True, False)
             else:
-                for j in range(GROUP_TILES + 1):
-                    if j < GROUP_TILES:
-                        nc.vector.scalar_tensor_tensor(
-                            out=value[:, j, :], in0=hid_banks[j][:], scalar=bias_hn[:, first + j : first + j + 1],
-                            in1=before[:, j, :], op0=ALU.add, op1=ALU.mult,
-                        )
-                    if j > 0:
-                        i = j - 1
-                        nc.vector.tensor_tensor(out=value[:, i, :], in0=value[:, i, :], in1=x_banks[i][:], op=ALU.add)
-                        nc.scalar.activation(out=value[:, i, :], in_=value[:, i, :], func=ACT.Tanh,
-                                             bias=bias_xn[:, first + i : first + i + 1], scale=1.0)
-                        nc.gpsimd.tensor_tensor(out=value[:, i, :], in0=value[:, i, :],
-                                                in1=hid_flipped[:, first + i, :], op=ALU.subtract)
-            return value
-
-        out_rows = out.rearrange("(p a) h -> p a h", a=ROW_SETS)
-
-        def turn_back_and_store(s, value):
-            group, gate = stages[s]
-            if gate != GATE_ORDER[-1]:
-                return
-            flipped_banks = []
-            for j in range(GROUP_TILES):
-                flipped = psum.tile([P, ROW_SETS, P], F32, name="flipped_product", tag="bank")
-                for a in range(ROW_SETS):
-                    nc.tensor.transpose(flipped[:, a, :], value[:, j, a * P : (a + 1) * P], identity[:])
-                flipped_banks.append(flipped)
-            for j in range(GROUP_TILES):
-                cols = slice((group * GROUP_TILES + j) * P, (group * GROUP_TILES + j + 1) * P)
-                result = result_pool.tile([P, ROW_SETS, P], F32)
-                nc.vector.tensor_tensor(out=result[:], in0=flipped_banks[j][:], in1=hid_rows[:, :, cols], op=ALU.add)
-                nc.sync.dma_start(out=out_rows[:, :, cols], in_=result[:])
-
-        wh_mx = {0: quantise_wh(0)}
-        values = {}
-        for s in range(len(stages)):
-            if s + 1 < len(stages):
-                wh_mx[s + 1] = quantise_wh(s + 1)
-            banks = multiply(s, wh_mx[s])
-            if s > 0:
-                turn_back_and_store(s - 1, values[s - 1])
-            values[s] = gate_arithmetic(s, banks, values.get(s - 1))
-        turn_back_and_store(len(stages) - 1, values[len(stages) - 1])
+                x_half(r_bank, GATE_R, group, True, False)
+                for j in tiles_of(group - 1):
+                    flip_z(j)
+            prepare(GATE_N, group)
+            if group == 0:
+                x_half(r_bank, GATE_R, group, False, True)
+            else:
+                hid_half(r_bank, GATE_R, group, False, True)
+            for j in tiles_of(group):
+                sigmoid_r(j)
+            if group > 0:
+                for j in tiles_of(group - 1):
+                    step_e(j)
+            hid_half(nh_bank, GATE_N, group, True, True)
+            for j in tiles_of(group):
+                step_t(j)
+            x_half(nx_bank, GATE_N, group, True, True)
+            prepare(GATE_Z, group)
+            for j in tiles_of(group):
+                step_y(j)
+            if group + 1 < GROUPS:
+                prepare(GATE_R, group + 1)
+            if group > 0:
+                for j in tiles_of(group - 1):
+                    finish(j)
+            x_half(z_bank, GATE_Z, group, True, False)
+            for j in tiles_of(group):
+                flip_y(j)
+            for j in tiles_of(group):
+                tanh_n(j)
+                step_d(j)
+            if group + 1 < GROUPS:
+                hid_half(z_bank, GATE_Z, group, False, True)
+                for j in tiles_of(group):
+                    sigmoid_z(j)
+        last = GROUPS - 1
+        for j in tiles_of(last):
+            for c in range(PASSES):
+                hid_pass(z_bank[j], GATE_Z, j, c, False, c == PASSES - 1)
+            sigmoid_z(j)
+            if j > last * GROUP_TILES:
+                flip_z(j - 1)
+                step_e(j - 1)
+            if j > last * GROUP_TILES + 1:
+                finish(j - 2)
+        flip_z(TILES - 1)
+        step_e(TILES - 1)
+        finish(TILES - 2)
+        finish(TILES - 1)

@@ -27,7 +27,7 @@ TILES = FEATURES // P
 
 RUN = 4
 RUNS_ALL = GROUP_COLS // RUN
-VECTOR_SHARE = {(0, 0): 64, (2, 0): 64, (1, 0): 64, (0, 1): 64, (2, 1): 128, (1, 1): 64}
+VECTOR_SHARE = {(0, 0): 64, (2, 0): 64, (1, 0): 32, (0, 1): 32, (2, 1): 96, (1, 1): 32}
 
 FLOPS = 2 * BATCH * (K_DIM + K_DIM) * 3 * FEATURES
 
@@ -219,7 +219,7 @@ def tile_grucellv2_e_kernel(tc, x, hid, wx_words, wx_scales, wh, bx, bh, out):
             nc.scalar.activation(out=n_value[j][:], in_=y_flipped[j][:], func=ACT.Tanh)
 
         def step_d(j):
-            engine = nc.gpsimd
+            engine = nc.vector if j in range(TILES) else nc.gpsimd
             engine.tensor_tensor(out=n_value[j][:], in0=n_value[j][:], in1=hid_rows[:, :, j * P : (j + 1) * P], op=ALU.subtract)
 
         def sigmoid_z(j):
@@ -235,7 +235,7 @@ def tile_grucellv2_e_kernel(tc, x, hid, wx_words, wx_scales, wh, bx, bh, out):
 
         def finish(j):
             cols = slice(j * P, (j + 1) * P)
-            engine = nc.vector
+            engine = nc.gpsimd if j in () else nc.vector
             engine.tensor_tensor(out=results[j][:], in0=results[j][:], in1=hid_rows[:, :, cols], op=ALU.add)
             nc.sync.dma_start(out=out_rows[:, :, cols], in_=results[j][:])
 

@@ -45,6 +45,8 @@ def tile_grucellv2_e_kernel(tc, x, hid, wx_words, wx_scales, wh, bx, bh, out):
         psum = ctx.enter_context(tc.psum_pool(name="psum", bufs=8))
         ctx.enter_context(tc.manual_schedule())
 
+        idle = consts.tile([P, BATCH], BF16)
+        nc.gpsimd.memset(idle[:], 0.0)
         warm = consts.tile([P, 2], F32)
         nc.vector.memset(warm[:], 0.0)
         nc.scalar.activation(out=warm[:, 1:2], in_=warm[:, 0:1], func=ACT.Sigmoid)
@@ -84,13 +86,13 @@ def tile_grucellv2_e_kernel(tc, x, hid, wx_words, wx_scales, wh, bx, bh, out):
 
         wh_raw = {}
 
-        def load_wh(gate, group):
+        def load_wh(gate, group, cs=range(PASSES)):
             cols = slice(group * GROUP_COLS, (group + 1) * GROUP_COLS)
-            for c in range(PASSES):
+            for c in cs:
                 raw = raw_pool.tile([P, PACK, GROUP_COLS], BF16)
                 rows = wh[gate, c * K_PASS : (c + 1) * K_PASS, cols]
                 nc.sync.dma_start(out=raw[:], in_=rows.rearrange("(p t) n -> p t n", t=PACK))
-                wh_raw[(gate, c, group)] = raw
+                wh_raw[(gate, c, group)] = raw[:]
 
         load_rows(hid_rows, hid)
         load_rows(x_rows, x)
@@ -111,32 +113,36 @@ def tile_grucellv2_e_kernel(tc, x, hid, wx_words, wx_scales, wh, bx, bh, out):
         identity_bf16 = consts.tile([P, P], BF16)
         make_identity(nc, identity_bf16[:])
 
-        def flip_rows(rows_tile, label):
-            words = rows_tile[:].bitcast(F32)
-            grouped = resident.tile([P, PASSES, BATCH * PACK], BF16, align_bytes=64, name=label + "_grouped")
-            grouped_words = grouped[:].bitcast(F32).rearrange("p c (b u) -> p c b u", u=2)
-            half = K_PASS // 2
-            for a in range(ROW_SETS):
-                flipped = psum.tile([P, PASSES, 2, P], F32, tag="bank")
-                for c in range(PASSES):
-                    for u in range(2):
-                        nc.tensor.transpose(flipped[:, c, u, :], words[:, a, c * half + u : (c + 1) * half : 2], identity[:])
-                copy_out = nc.vector.tensor_copy if a % 2 == 1 else nc.scalar.copy
-                copy_out(out=grouped_words[:, :, a * P : (a + 1) * P, :], in_=flipped[:].rearrange("p c u b -> p c b u"))
-            return grouped
+        def new_grouped(label):
+            return resident.tile([P, PASSES, BATCH * PACK], BF16, align_bytes=64, name=label + "_grouped")
 
-        def quantise_rows(grouped, label):
+        def flip_set(rows_tile, a):
+            words = rows_tile[:].bitcast(F32)
+            half = K_PASS // 2
+            flipped = psum.tile([P, PASSES, 2, P], F32, name="flipped", tag="bank")
+            for c in range(PASSES):
+                for u in range(2):
+                    nc.tensor.transpose(flipped[:, c, u, :], words[:, a, c * half + u : (c + 1) * half : 2], identity[:])
+            return flipped
+
+        def copy_set(flipped, grouped, a):
+            grouped_words = grouped[:].bitcast(F32).rearrange("p c (b u) -> p c b u", u=2)
+            copy_out = nc.vector.tensor_copy if a % 2 == 1 else nc.scalar.copy
+            copy_out(out=grouped_words[:, :, a * P : (a + 1) * P, :], in_=flipped[:].rearrange("p c u b -> p c b u"))
+
+        def new_codes(label):
             codes = resident.tile([P, PASSES, BATCH], U32, align_bytes=64, name=label + "_codes")
             scales = resident.tile([P, PASSES, BATCH], U8, align_bytes=64, name=label + "_scales")
-            for c in range(PASSES):
-                nc.vector.quantize_mx(out=codes[:, c, :].bitcast(FP8X4), scales=scales[:, c, :], in_=grouped[:, c, :])
-            return codes[:], scales[:]
+            return codes, scales
+
+        def quantise_half(grouped, codes, scales, c):
+            nc.vector.quantize_mx(out=codes[:, c, :].bitcast(FP8X4), scales=scales[:, c, :], in_=grouped[:, c, :])
 
         wh_codes, wh_scales, wh_grouped = {}, {}, {}
 
         def regroup(gate, c, group):
             grouped = grouped_pool.tile([P, GROUP_COLS, PACK], BF16, align_bytes=64)
-            src = wh_raw[(gate, c, group)][:].rearrange("p t (n i) -> p n t i", i=RUN)
+            src = wh_raw[(gate, c, group)].rearrange("p t (n i) -> p n t i", i=RUN)
             dst = grouped[:].rearrange("p (n i) t -> p n t i", i=RUN)
             runs = VECTOR_SHARE[(gate, group)]
             if runs > 0:
@@ -159,6 +165,11 @@ def tile_grucellv2_e_kernel(tc, x, hid, wx_words, wx_scales, wh, bx, bh, out):
             for c in range(PASSES):
                 regroup(gate, c, group)
             for c in range(PASSES):
+                quantise(gate, c, group)
+
+        def prepare_in_turn(gate, group):
+            for c in range(PASSES):
+                regroup(gate, c, group)
                 quantise(gate, c, group)
 
         def new_bank():
@@ -235,9 +246,15 @@ def tile_grucellv2_e_kernel(tc, x, hid, wx_words, wx_scales, wh, bx, bh, out):
 
         def finish(j):
             cols = slice(j * P, (j + 1) * P)
-            engine = nc.gpsimd if j in () else nc.vector
+            engine = nc.gpsimd if j in (0,1,2,3,4,5) else nc.vector
             engine.tensor_tensor(out=results[j][:], in0=results[j][:], in1=hid_rows[:, :, cols], op=ALU.add)
             nc.sync.dma_start(out=out_rows[:, :, cols], in_=results[j][:])
+
+        idle_bank = psum.tile([P, BATCH], F32, name="idle_bank", tag="bank")
+
+        def keep_warm(n):
+            for i in range(n):
+                nc.tensor.matmul(idle_bank[:], lhsT=idle[:, 0:P], rhs=idle[:], start=True, stop=True)
 
         def x_half(banks, gate, group, start, stop):
             for j in tiles_of(group):
@@ -253,11 +270,22 @@ def tile_grucellv2_e_kernel(tc, x, hid, wx_words, wx_scales, wh, bx, bh, out):
                 for c in range(PASSES):
                     hid_pass(banks[j], gate, j, c, start and c == 0, stop and c == PASSES - 1)
 
-        hid_grouped = flip_rows(hid_rows, "hid")
-        hid_codes, hid_scales = quantise_rows(hid_grouped, "hid")
+        keep_warm(4)
+        hid_grouped = new_grouped("hid")
+        hid_codes, hid_scales = new_codes("hid")
+        x_grouped = new_grouped("x")
+        x_codes, x_scales = new_codes("x")
+        for a in range(ROW_SETS):
+            copy_set(flip_set(hid_rows, a), hid_grouped, a)
+            keep_warm(1)
+        for c in range(PASSES):
+            quantise_half(hid_grouped, hid_codes, hid_scales, c)
         prepare(GATE_R, 0)
-        x_grouped = flip_rows(x_rows, "x")
-        x_codes, x_scales = quantise_rows(x_grouped, "x")
+        for a in range(ROW_SETS):
+            copy_set(flip_set(x_rows, a), x_grouped, a)
+            keep_warm(1)
+        for c in range(PASSES):
+            quantise_half(x_grouped, x_codes, x_scales, c)
         bias_bank = psum.tile([P, P], BF16, tag="bank")
         nc.tensor.transpose(bias_bank[:], bias_rows[:], identity_bf16[:])
         bias_cols = consts.tile([P, 64], F32)
@@ -275,10 +303,12 @@ def tile_grucellv2_e_kernel(tc, x, hid, wx_words, wx_scales, wh, bx, bh, out):
         bias_xn = bias_of(0, GATE_N)
         bias_hn = bias_of(32, GATE_N)
 
+        for j in tiles_of(0):
+            r_bank[j] = new_bank()
+            for c in range(PASSES):
+                hid_pass(r_bank[j], GATE_R, j, c, c == 0, False)
         for group in range(GROUPS):
-            if group == 0:
-                hid_half(r_bank, GATE_R, group, True, False)
-            else:
+            if group > 0:
                 x_half(r_bank, GATE_R, group, True, False)
                 for j in tiles_of(group - 1):
                     flip_z(j)
@@ -292,6 +322,7 @@ def tile_grucellv2_e_kernel(tc, x, hid, wx_words, wx_scales, wh, bx, bh, out):
             if group > 0:
                 for j in tiles_of(group - 1):
                     step_e(j)
+                    finish(j)
             hid_half(nh_bank, GATE_N, group, True, True)
             for j in tiles_of(group):
                 step_t(j)
@@ -301,9 +332,6 @@ def tile_grucellv2_e_kernel(tc, x, hid, wx_words, wx_scales, wh, bx, bh, out):
                 step_y(j)
             if group + 1 < GROUPS:
                 prepare(GATE_R, group + 1)
-            if group > 0:
-                for j in tiles_of(group - 1):
-                    finish(j)
             x_half(z_bank, GATE_Z, group, True, False)
             for j in tiles_of(group):
                 flip_y(j)
@@ -318,13 +346,11 @@ def tile_grucellv2_e_kernel(tc, x, hid, wx_words, wx_scales, wh, bx, bh, out):
         for j in tiles_of(last):
             for c in range(PASSES):
                 hid_pass(z_bank[j], GATE_Z, j, c, False, c == PASSES - 1)
+        for j in tiles_of(last):
             sigmoid_z(j)
+            flip_z(j)
+        for j in tiles_of(last):
+            step_e(j)
             if j > last * GROUP_TILES:
-                flip_z(j - 1)
-                step_e(j - 1)
-            if j > last * GROUP_TILES + 1:
-                finish(j - 2)
-        flip_z(TILES - 1)
-        step_e(TILES - 1)
-        finish(TILES - 2)
+                finish(j - 1)
         finish(TILES - 1)

@@ -25,6 +25,7 @@ GROUP_COLS = FEATURES // GROUPS
 GROUP_TILES = GROUP_COLS // P
 TILES = FEATURES // P
 
+V_SETS = 0
 RUN = 4
 RUNS_ALL = GROUP_COLS // RUN
 VECTOR_SHARE = {(0, 0): 64, (2, 0): 64, (1, 0): 32, (0, 1): 32, (2, 1): 96, (1, 1): 32}
@@ -114,7 +115,10 @@ def tile_grucellv2_e_kernel(tc, x, hid, wx_words, wx_scales, wh, bx, bh, out):
         make_identity(nc, identity_bf16[:])
 
         def new_grouped(label):
-            return resident.tile([P, PASSES, BATCH * PACK], BF16, align_bytes=64, name=label + "_grouped")
+            return [
+                resident.tile([P, PASSES, BATCH * PACK // 2], BF16, align_bytes=64, name="%s_grouped_%d" % (label, side))
+                for side in range(2)
+            ]
 
         def flip_set(rows_tile, a):
             words = rows_tile[:].bitcast(F32)
@@ -126,17 +130,23 @@ def tile_grucellv2_e_kernel(tc, x, hid, wx_words, wx_scales, wh, bx, bh, out):
             return flipped
 
         def copy_set(flipped, grouped, a):
-            grouped_words = grouped[:].bitcast(F32).rearrange("p c (b u) -> p c b u", u=2)
-            copy_out = nc.vector.tensor_copy if a % 2 == 1 else nc.scalar.copy
-            copy_out(out=grouped_words[:, :, a * P : (a + 1) * P, :], in_=flipped[:].rearrange("p c u b -> p c b u"))
+            side, i = divmod(a, 2)
+            grouped_words = grouped[side][:].bitcast(F32).rearrange("p c (b u) -> p c b u", u=2)
+            copy_out = nc.vector.tensor_copy if a % 2 == V_SETS else nc.scalar.copy
+            copy_out(out=grouped_words[:, :, i * P : (i + 1) * P, :], in_=flipped[:].rearrange("p c u b -> p c b u"))
 
         def new_codes(label):
             codes = resident.tile([P, PASSES, BATCH], U32, align_bytes=64, name=label + "_codes")
             scales = resident.tile([P, PASSES, BATCH], U8, align_bytes=64, name=label + "_scales")
             return codes, scales
 
-        def quantise_half(grouped, codes, scales, c):
-            nc.vector.quantize_mx(out=codes[:, c, :].bitcast(FP8X4), scales=scales[:, c, :], in_=grouped[:, c, :])
+        def quantise_rows(grouped, codes, scales, side):
+            cols = slice(side * BATCH // 2, (side + 1) * BATCH // 2)
+            for c in range(PASSES):
+                nc.vector.quantize_mx(
+                    out=codes[:, c, cols].bitcast(FP8X4), scales=scales[:, c, cols],
+                    in_=grouped[side][:, c, :],
+                )
 
         wh_codes, wh_scales, wh_grouped = {}, {}, {}
 
@@ -167,11 +177,6 @@ def tile_grucellv2_e_kernel(tc, x, hid, wx_words, wx_scales, wh, bx, bh, out):
             for c in range(PASSES):
                 quantise(gate, c, group)
 
-        def prepare_in_turn(gate, group):
-            for c in range(PASSES):
-                regroup(gate, c, group)
-                quantise(gate, c, group)
-
         def new_bank():
             return psum.tile([P, BATCH], F32, name="bank", tag="bank")
 
@@ -199,7 +204,7 @@ def tile_grucellv2_e_kernel(tc, x, hid, wx_words, wx_scales, wh, bx, bh, out):
         r_bank, nh_bank, nx_bank, z_bank, y_flipped, z_flipped = {}, {}, {}, {}, {}, {}
 
         def sigmoid_r(j):
-            r_value[j] = gate_pool.tile([P, BATCH], F32, name="r_value")
+            r_value[j] = gate_pool.tile([P, BATCH], F32, name="r_value", bufs=TILES)
             nc.scalar.activation(out=r_value[j][:], in_=r_bank[j][:], func=ACT.Sigmoid, bias=bias_r[:, j : j + 1], scale=1.0)
 
         def step_t(j):
@@ -250,12 +255,6 @@ def tile_grucellv2_e_kernel(tc, x, hid, wx_words, wx_scales, wh, bx, bh, out):
             engine.tensor_tensor(out=results[j][:], in0=results[j][:], in1=hid_rows[:, :, cols], op=ALU.add)
             nc.sync.dma_start(out=out_rows[:, :, cols], in_=results[j][:])
 
-        idle_bank = psum.tile([P, BATCH], F32, name="idle_bank", tag="bank")
-
-        def keep_warm(n):
-            for i in range(n):
-                nc.tensor.matmul(idle_bank[:], lhsT=idle[:, 0:P], rhs=idle[:], start=True, stop=True)
-
         def x_half(banks, gate, group, start, stop):
             for j in tiles_of(group):
                 if start:
@@ -270,27 +269,32 @@ def tile_grucellv2_e_kernel(tc, x, hid, wx_words, wx_scales, wh, bx, bh, out):
                 for c in range(PASSES):
                     hid_pass(banks[j], gate, j, c, start and c == 0, stop and c == PASSES - 1)
 
-        keep_warm(4)
         hid_grouped = new_grouped("hid")
         hid_codes, hid_scales = new_codes("hid")
         x_grouped = new_grouped("x")
         x_codes, x_scales = new_codes("x")
-        for a in range(ROW_SETS):
-            copy_set(flip_set(hid_rows, a), hid_grouped, a)
-            keep_warm(1)
-        for c in range(PASSES):
-            quantise_half(hid_grouped, hid_codes, hid_scales, c)
-        prepare(GATE_R, 0)
-        for a in range(ROW_SETS):
-            copy_set(flip_set(x_rows, a), x_grouped, a)
-            keep_warm(1)
-        for c in range(PASSES):
-            quantise_half(x_grouped, x_codes, x_scales, c)
+        hid_flipped = [flip_set(hid_rows, a) for a in range(ROW_SETS)]
+        x_flipped = [flip_set(x_rows, a) for a in range(ROW_SETS)]
         bias_bank = psum.tile([P, P], BF16, tag="bank")
         nc.tensor.transpose(bias_bank[:], bias_rows[:], identity_bf16[:])
+        idle_bank = psum.tile([P, BATCH], F32, tag="bank")
+        for i in range(4):
+            nc.tensor.matmul(idle_bank[:], lhsT=idle[:, 0:P], rhs=idle[:], start=True, stop=True)
+        for a in range(3):
+            copy_set(hid_flipped[a], hid_grouped, a)
+        quantise_rows(hid_grouped, hid_codes, hid_scales, 0)
+        copy_set(hid_flipped[3], hid_grouped, 3)
+        quantise_rows(hid_grouped, hid_codes, hid_scales, 1)
+        copy_set(x_flipped[0], x_grouped, 0)
+        copy_set(x_flipped[1], x_grouped, 1)
+        regroup(GATE_R, 0, 0)
+        copy_set(x_flipped[2], x_grouped, 2)
+        copy_set(x_flipped[3], x_grouped, 3)
         bias_cols = consts.tile([P, 64], F32)
         nc.vector.tensor_copy(out=bias_cols[:], in_=bias_bank[:, 0:64])
 
+        quantise(GATE_R, 0, 0)
+        quantise_rows(x_grouped, x_codes, x_scales, 0)
         def bias_of(first_row, gate):
             return bias_cols[:, first_row + gate * TILES : first_row + (gate + 1) * TILES]
 
@@ -303,19 +307,25 @@ def tile_grucellv2_e_kernel(tc, x, hid, wx_words, wx_scales, wh, bx, bh, out):
         bias_xn = bias_of(0, GATE_N)
         bias_hn = bias_of(32, GATE_N)
 
+        regroup(GATE_R, 1, 0)
+        quantise_rows(x_grouped, x_codes, x_scales, 1)
+        quantise(GATE_R, 1, 0)
         for j in tiles_of(0):
             r_bank[j] = new_bank()
-            for c in range(PASSES):
-                hid_pass(r_bank[j], GATE_R, j, c, c == 0, False)
+        for j in tiles_of(0):
+            hid_pass(r_bank[j], GATE_R, j, 0, True, False)
+        for c in range(PASSES):
+            for j in tiles_of(0):
+                x_pass(r_bank[j], GATE_R, j, c, False, False)
+        for j in tiles_of(0):
+            hid_pass(r_bank[j], GATE_R, j, 1, False, True)
         for group in range(GROUPS):
             if group > 0:
                 x_half(r_bank, GATE_R, group, True, False)
                 for j in tiles_of(group - 1):
                     flip_z(j)
             prepare(GATE_N, group)
-            if group == 0:
-                x_half(r_bank, GATE_R, group, False, True)
-            else:
+            if group > 0:
                 hid_half(r_bank, GATE_R, group, False, True)
             for j in tiles_of(group):
                 sigmoid_r(j)
@@ -327,9 +337,9 @@ def tile_grucellv2_e_kernel(tc, x, hid, wx_words, wx_scales, wh, bx, bh, out):
             for j in tiles_of(group):
                 step_t(j)
             x_half(nx_bank, GATE_N, group, True, True)
-            prepare(GATE_Z, group)
             for j in tiles_of(group):
                 step_y(j)
+            prepare(GATE_Z, group)
             if group + 1 < GROUPS:
                 prepare(GATE_R, group + 1)
             x_half(z_bank, GATE_Z, group, True, False)

@@ -235,7 +235,7 @@ def tile_grucellv2_e_kernel(tc, x, hid, wx_words, wx_scales, wh, bx, bh, out):
             nc.scalar.activation(out=n_value[j][:], in_=y_flipped[j][:], func=ACT.Tanh)
 
         def step_d(j):
-            engine = nc.vector if j in range(TILES) else nc.gpsimd
+            engine = nc.vector if j in (0, 1, 2, 3, 4, 5) else nc.gpsimd
             engine.tensor_tensor(out=n_value[j][:], in0=n_value[j][:], in1=hid_rows[:, :, j * P : (j + 1) * P], op=ALU.subtract)
 
         def sigmoid_z(j):
@@ -251,9 +251,30 @@ def tile_grucellv2_e_kernel(tc, x, hid, wx_words, wx_scales, wh, bx, bh, out):
 
         def finish(j):
             cols = slice(j * P, (j + 1) * P)
-            engine = nc.gpsimd if j in (0,1,2,3,4,5) else nc.vector
+            engine = nc.gpsimd if j in (0, 1, 2, 3) else nc.vector
             engine.tensor_tensor(out=results[j][:], in0=results[j][:], in1=hid_rows[:, :, cols], op=ALU.add)
             nc.sync.dma_start(out=out_rows[:, :, cols], in_=results[j][:])
+
+        def sigmoid_z_half(j, side):
+            cols = slice(side * BATCH // 2, (side + 1) * BATCH // 2)
+            nc.scalar.activation(out=z_value[j][:, cols], in_=z_bank[j][:, cols], func=ACT.Sigmoid, bias=minus_bias_z[:, j : j + 1], scale=-1.0)
+
+        def flip_z_half(j, side):
+            flipped = psum.tile([P, 2, P], F32, name="z_half", tag="bank")
+            for i in range(2):
+                a = 2 * side + i
+                nc.tensor.transpose(flipped[:, i, :], z_value[j][:, a * P : (a + 1) * P], identity[:])
+            z_flipped[(j, side)] = flipped
+
+        def step_e_half(j, side):
+            sets = slice(2 * side, 2 * side + 2)
+            nc.vector.tensor_tensor(out=results[j][:, sets, :], in0=z_flipped[(j, side)][:], in1=n_value[j][:, sets, :], op=ALU.mult)
+
+        def finish_half(j, side):
+            sets = slice(2 * side, 2 * side + 2)
+            cols = slice(j * P, (j + 1) * P)
+            nc.vector.tensor_tensor(out=results[j][:, sets, :], in0=results[j][:, sets, :], in1=hid_rows[:, sets, cols], op=ALU.add)
+            nc.sync.dma_start(out=out_rows[:, sets, cols], in_=results[j][:, sets, :])
 
         def x_half(banks, gate, group, start, stop):
             for j in tiles_of(group):
@@ -337,30 +358,62 @@ def tile_grucellv2_e_kernel(tc, x, hid, wx_words, wx_scales, wh, bx, bh, out):
             for j in tiles_of(group):
                 step_t(j)
             x_half(nx_bank, GATE_N, group, True, True)
+            if group == GROUPS - 1:
+                prepare(GATE_Z, group)
             for j in tiles_of(group):
                 step_y(j)
-            prepare(GATE_Z, group)
-            if group + 1 < GROUPS:
-                prepare(GATE_R, group + 1)
+            if group < GROUPS - 1:
+                prepare(GATE_Z, group)
+            if group == GROUPS - 1:
+                break
+            prepare(GATE_R, group + 1)
             x_half(z_bank, GATE_Z, group, True, False)
             for j in tiles_of(group):
                 flip_y(j)
             for j in tiles_of(group):
                 tanh_n(j)
                 step_d(j)
-            if group + 1 < GROUPS:
-                hid_half(z_bank, GATE_Z, group, False, True)
-                for j in tiles_of(group):
-                    sigmoid_z(j)
-        last = GROUPS - 1
-        for j in tiles_of(last):
+            hid_half(z_bank, GATE_Z, group, False, True)
+            for j in tiles_of(group):
+                sigmoid_z(j)
+        first, second, third, fourth = tiles_of(GROUPS - 1)
+
+        def all_passes(j):
+            z_bank[j] = new_bank()
+            for c in range(PASSES):
+                x_pass(z_bank[j], GATE_Z, j, c, c == 0, False)
             for c in range(PASSES):
                 hid_pass(z_bank[j], GATE_Z, j, c, False, c == PASSES - 1)
-        for j in tiles_of(last):
-            sigmoid_z(j)
-            flip_z(j)
-        for j in tiles_of(last):
-            step_e(j)
-            if j > last * GROUP_TILES:
-                finish(j - 1)
-        finish(TILES - 1)
+
+        all_passes(first)
+        sigmoid_z(first)
+        all_passes(second)
+        sigmoid_z(second)
+        for j in tiles_of(GROUPS - 1):
+            flip_y(j)
+            tanh_n(j)
+        flip_z(first)
+        flip_z(second)
+        all_passes(third)
+        sigmoid_z(third)
+        all_passes(fourth)
+        z_value[fourth] = gate_pool.tile([P, BATCH], F32, name="z_value", bufs=GROUP_TILES)
+        results[fourth] = result_pool.tile([P, ROW_SETS, P], F32, name="result")
+        flip_z(third)
+        for side in range(2):
+            sigmoid_z_half(fourth, side)
+            flip_z_half(fourth, side)
+        step_d(first)
+        step_d(second)
+        step_d(third)
+        step_d(fourth)
+        step_e(first)
+        step_e(second)
+        finish(first)
+        finish(second)
+        step_e(third)
+        step_e_half(fourth, 0)
+        finish(third)
+        step_e_half(fourth, 1)
+        finish_half(fourth, 0)
+        finish_half(fourth, 1)

@@ -65,7 +65,7 @@ def tile_grucellv2_e_kernel(tc, x, hid, wx_words, wx_scales, wh, bx, bh, out):
             for a in range(ROW_SETS):
                 nc.sync.dma_start(out=rows_tile[:, a, :], in_=by_partition[:, a, :])
 
-        wx_planes = resident.tile([P, 3 * PASSES, FEATURES], U8, align_bytes=64)
+        wx_planes = resident.tile([P, 3 * PASSES, FEATURES], U8, align_bytes=256)
         scale_rows = wx_scales.rearrange("g (quad r) n -> r quad g n", r=4)
 
         def load_planes(planes):
@@ -77,7 +77,7 @@ def tile_grucellv2_e_kernel(tc, x, hid, wx_words, wx_scales, wh, bx, bh, out):
         nc.vector.memset(wx_planes[:, first_planes, :].bitcast(I32), 0)
         nc.vector.memset(wx_planes[:, later_planes, :].bitcast(I32), 0)
 
-        wx_codes = resident.tile([P, 3 * PASSES, FEATURES], U32, align_bytes=64)
+        wx_codes = resident.tile([P, 3 * PASSES, FEATURES], U32, align_bytes=256)
         wx_words_by_partition = wx_words.rearrange("g p n t -> p g (n t)").bitcast(I32)
 
         def load_wx(gate, group):
@@ -116,7 +116,7 @@ def tile_grucellv2_e_kernel(tc, x, hid, wx_words, wx_scales, wh, bx, bh, out):
 
         def new_grouped(label):
             return [
-                resident.tile([P, PASSES, BATCH * PACK // 2], BF16, align_bytes=64, name="%s_grouped_%d" % (label, side))
+                resident.tile([P, PASSES, BATCH * PACK // 2], BF16, align_bytes=256, name="%s_grouped_%d" % (label, side))
                 for side in range(2)
             ]
 
@@ -136,8 +136,8 @@ def tile_grucellv2_e_kernel(tc, x, hid, wx_words, wx_scales, wh, bx, bh, out):
             copy_out(out=grouped_words[:, :, i * P : (i + 1) * P, :], in_=flipped[:].rearrange("p c u b -> p c b u"))
 
         def new_codes(label):
-            codes = resident.tile([P, PASSES, BATCH], U32, align_bytes=64, name=label + "_codes")
-            scales = resident.tile([P, PASSES, BATCH], U8, align_bytes=64, name=label + "_scales")
+            codes = resident.tile([P, PASSES, BATCH], U32, align_bytes=256, name=label + "_codes")
+            scales = resident.tile([P, PASSES, BATCH], U8, align_bytes=256, name=label + "_scales")
             return codes, scales
 
         def quantise_rows(grouped, codes, scales, side):
@@ -151,7 +151,7 @@ def tile_grucellv2_e_kernel(tc, x, hid, wx_words, wx_scales, wh, bx, bh, out):
         wh_codes, wh_scales, wh_grouped = {}, {}, {}
 
         def regroup(gate, c, group):
-            grouped = grouped_pool.tile([P, GROUP_COLS, PACK], BF16, align_bytes=64)
+            grouped = grouped_pool.tile([P, GROUP_COLS, PACK], BF16, align_bytes=256)
             src = wh_raw[(gate, c, group)].rearrange("p t (n i) -> p n t i", i=RUN)
             dst = grouped[:].rearrange("p (n i) t -> p n t i", i=RUN)
             runs = VECTOR_SHARE[(gate, group)]
@@ -162,8 +162,8 @@ def tile_grucellv2_e_kernel(tc, x, hid, wx_words, wx_scales, wh, bx, bh, out):
             wh_grouped[(gate, c, group)] = grouped
 
         def quantise(gate, c, group):
-            codes = resident.tile([P, GROUP_COLS], U32, align_bytes=64, name="wh_codes_%d_%d_%d" % (gate, c, group))
-            scales = resident.tile([P, GROUP_COLS], U8, align_bytes=64, name="wh_scales_%d_%d_%d" % (gate, c, group))
+            codes = resident.tile([P, GROUP_COLS], U32, align_bytes=256, name="wh_codes_%d_%d_%d" % (gate, c, group))
+            scales = resident.tile([P, GROUP_COLS], U8, align_bytes=256, name="wh_scales_%d_%d_%d" % (gate, c, group))
             nc.vector.quantize_mx(
                 out=codes[:].bitcast(FP8X4), scales=scales[:],
                 in_=wh_grouped[(gate, c, group)][:].rearrange("p n t -> p (n t)"),

@@ -26,9 +26,9 @@ GROUP_TILES = GROUP_COLS // P
 TILES = FEATURES // P
 
 V_SETS = 0
-RUN = 4
+RUN = 8
 RUNS_ALL = GROUP_COLS // RUN
-VECTOR_SHARE = {(0, 0): 64, (2, 0): 64, (1, 0): 32, (0, 1): 32, (2, 1): 96, (1, 1): 32}
+VECTOR_SHARE = {(0, 0): 32, (2, 0): 32, (1, 0): 16, (0, 1): 16, (2, 1): 48, (1, 1): 16}
 
 FLOPS = 2 * BATCH * (K_DIM + K_DIM) * 3 * FEATURES
 

@@ -26,6 +26,7 @@ GROUP_TILES = GROUP_COLS // P
 TILES = FEATURES // P
 
 V_SETS = 0
+EARLY_ADDS = (0, 1, 2)
 RUN = 8
 RUNS_ALL = GROUP_COLS // RUN
 VECTOR_SHARE = {(0, 0): 32, (2, 0): 32, (1, 0): 16, (0, 1): 16, (2, 1): 48, (1, 1): 16}
@@ -76,6 +77,9 @@ def tile_grucellv2_e_kernel(tc, x, hid, wx_words, wx_scales, wh, bx, bh, out):
         later_planes = slice(PASSES, 3 * PASSES)
         nc.vector.memset(wx_planes[:, first_planes, :].bitcast(I32), 0)
         nc.vector.memset(wx_planes[:, later_planes, :].bitcast(I32), 0)
+
+        def load_gate_planes(gate):
+            load_planes(slice(gate * PASSES, (gate + 1) * PASSES))
 
         wx_codes = resident.tile([P, 3 * PASSES, FEATURES], U32, align_bytes=256)
         wx_words_by_partition = wx_words.rearrange("g p n t -> p g (n t)").bitcast(I32)
@@ -235,7 +239,7 @@ def tile_grucellv2_e_kernel(tc, x, hid, wx_words, wx_scales, wh, bx, bh, out):
             nc.scalar.activation(out=n_value[j][:], in_=y_flipped[j][:], func=ACT.Tanh)
 
         def step_d(j):
-            engine = nc.vector if j in (0, 1, 2, 3, 4, 5) else nc.gpsimd
+            engine = nc.vector if j in (0, 1, 2, 3, 4, 5, 6) else nc.gpsimd
             engine.tensor_tensor(out=n_value[j][:], in0=n_value[j][:], in1=hid_rows[:, :, j * P : (j + 1) * P], op=ALU.subtract)
 
         def sigmoid_z(j):
@@ -251,7 +255,7 @@ def tile_grucellv2_e_kernel(tc, x, hid, wx_words, wx_scales, wh, bx, bh, out):
 
         def finish(j):
             cols = slice(j * P, (j + 1) * P)
-            engine = nc.gpsimd if j in (0, 1, 2, 3) else nc.vector
+            engine = nc.gpsimd if j in (0, 1, 2) else nc.vector
             engine.tensor_tensor(out=results[j][:], in0=results[j][:], in1=hid_rows[:, :, cols], op=ALU.add)
             nc.sync.dma_start(out=out_rows[:, :, cols], in_=results[j][:])
 
@@ -353,7 +357,8 @@ def tile_grucellv2_e_kernel(tc, x, hid, wx_words, wx_scales, wh, bx, bh, out):
             if group > 0:
                 for j in tiles_of(group - 1):
                     step_e(j)
-                    finish(j)
+                    if j in EARLY_ADDS:
+                        finish(j)
             hid_half(nh_bank, GATE_N, group, True, True)
             for j in tiles_of(group):
                 step_t(j)
@@ -365,6 +370,9 @@ def tile_grucellv2_e_kernel(tc, x, hid, wx_words, wx_scales, wh, bx, bh, out):
             if group < GROUPS - 1:
                 prepare(GATE_Z, group)
             if group == GROUPS - 1:
+                for j in tiles_of(group - 1):
+                    if j not in EARLY_ADDS:
+                        finish(j)
                 break
             prepare(GATE_R, group + 1)
             x_half(z_bank, GATE_Z, group, True, False)

@@ -29,7 +29,7 @@ V_SETS = 0
 EARLY_ADDS = (0, 1, 2)
 RUN = 8
 RUNS_ALL = GROUP_COLS // RUN
-VECTOR_SHARE = {(0, 0): 32, (2, 0): 32, (1, 0): 16, (0, 1): 16, (2, 1): 48, (1, 1): 16}
+VECTOR_SHARE = {(0, 0): 32, (2, 0): 32, (1, 0): 16, (0, 1): 32, (2, 1): 48, (1, 1): 16}
 
 FLOPS = 2 * BATCH * (K_DIM + K_DIM) * 3 * FEATURES
 
@@ -78,9 +78,6 @@ def tile_grucellv2_e_kernel(tc, x, hid, wx_words, wx_scales, wh, bx, bh, out):
         nc.vector.memset(wx_planes[:, first_planes, :].bitcast(I32), 0)
         nc.vector.memset(wx_planes[:, later_planes, :].bitcast(I32), 0)
 
-        def load_gate_planes(gate):
-            load_planes(slice(gate * PASSES, (gate + 1) * PASSES))
-
         wx_codes = resident.tile([P, 3 * PASSES, FEATURES], U32, align_bytes=256)
         wx_words_by_partition = wx_words.rearrange("g p n t -> p g (n t)").bitcast(I32)
 
@@ -107,8 +104,8 @@ def tile_grucellv2_e_kernel(tc, x, hid, wx_words, wx_scales, wh, bx, bh, out):
         load_wh(GATE_N, 0)
         load_planes(later_planes)
         load_wx(GATE_N, 0)
-        load_wh(GATE_Z, 0)
         load_wx(GATE_Z, 0)
+        load_wh(GATE_Z, 0)
         for gate in (GATE_R, GATE_N, GATE_Z):
             load_wh(gate, 1)
             load_wx(gate, 1)
@@ -239,7 +236,7 @@ def tile_grucellv2_e_kernel(tc, x, hid, wx_words, wx_scales, wh, bx, bh, out):
             nc.scalar.activation(out=n_value[j][:], in_=y_flipped[j][:], func=ACT.Tanh)
 
         def step_d(j):
-            engine = nc.vector if j in (0, 1, 2, 3, 4, 5, 6) else nc.gpsimd
+            engine = nc.vector if j in (0,1,2,3,4,5,6) else nc.gpsimd
             engine.tensor_tensor(out=n_value[j][:], in0=n_value[j][:], in1=hid_rows[:, :, j * P : (j + 1) * P], op=ALU.subtract)
 
         def sigmoid_z(j):

from contextlib import ExitStack

import concourse.mybir as mybir
from concourse.masks import make_identity

F32 = mybir.dt.float32
BF16 = mybir.dt.bfloat16
I32 = mybir.dt.int32
U32 = mybir.dt.uint32
U8 = mybir.dt.uint8
FP8X4 = mybir.dt.float8_e4m3fn_x4
ACT = mybir.ActivationFunctionType
ALU = mybir.AluOpType

P = 128
PACK = 4
K_PASS = P * PACK
BATCH, K_DIM, FEATURES = 512, 1024, 1024
PASSES = K_DIM // K_PASS
ROW_SETS = BATCH // P
GATE_R, GATE_Z, GATE_N = 0, 1, 2

GROUPS = 2
GROUP_COLS = FEATURES // GROUPS
GROUP_TILES = GROUP_COLS // P
TILES = FEATURES // P

V_SETS = 0
EARLY_ADDS = (0, 1, 2)
RUN = 8
RUNS_ALL = GROUP_COLS // RUN
VECTOR_SHARE = {(0, 0): 32, (2, 0): 32, (1, 0): 16, (0, 1): 32, (2, 1): 48, (1, 1): 16}

FLOPS = 2 * BATCH * (K_DIM + K_DIM) * 3 * FEATURES


def tile_grucellv2_e_kernel(tc, x, hid, wx_words, wx_scales, wh, bx, bh, out):
    nc = tc.nc

    with ExitStack() as ctx:
        consts = ctx.enter_context(tc.tile_pool(name="consts", bufs=1))
        resident = ctx.enter_context(tc.tile_pool(name="resident", bufs=1))
        raw_pool = ctx.enter_context(tc.tile_pool(name="raw", bufs=3 * PASSES * GROUPS))
        grouped_pool = ctx.enter_context(tc.tile_pool(name="grouped", bufs=4))
        gate_pool = ctx.enter_context(tc.tile_pool(name="gates", bufs=GROUP_TILES))
        result_pool = ctx.enter_context(tc.tile_pool(name="result", bufs=4))
        psum = ctx.enter_context(tc.psum_pool(name="psum", bufs=8))
        ctx.enter_context(tc.manual_schedule())

        idle = consts.tile([P, BATCH], BF16)
        nc.gpsimd.memset(idle[:], 0.0)
        warm = consts.tile([P, 2], F32)
        nc.vector.memset(warm[:], 0.0)
        nc.scalar.activation(out=warm[:, 1:2], in_=warm[:, 0:1], func=ACT.Sigmoid)

        bias_rows = consts.tile([P, P], BF16)
        nc.vector.memset(bias_rows[:], 0.0)
        nc.scalar.dma_start(out=bias_rows[0 : 3 * TILES, :], in_=bx.rearrange("g (j p) -> (g j) p", p=P))
        nc.scalar.dma_start(out=bias_rows[32 : 32 + 3 * TILES, :], in_=bh.rearrange("g (j p) -> (g j) p", p=P))

        x_rows = resident.tile([P, ROW_SETS, K_DIM], BF16)
        hid_rows = resident.tile([P, ROW_SETS, K_DIM], BF16)

        def load_rows(rows_tile, source):
            by_partition = source.rearrange("(p a) k -> p a k", a=ROW_SETS)
            for a in range(ROW_SETS):
                nc.sync.dma_start(out=rows_tile[:, a, :], in_=by_partition[:, a, :])

        wx_planes = resident.tile([P, 3 * PASSES, FEATURES], U8, align_bytes=256)
        scale_rows = wx_scales.rearrange("g (quad r) n -> r quad g n", r=4)

        def load_planes(planes):
            for r in range(4):
                nc.sync.dma_start(out=wx_planes[r:P:32, planes, :].bitcast(I32), in_=scale_rows[r][:, planes, :].bitcast(I32))

        first_planes = slice(0, PASSES)
        later_planes = slice(PASSES, 3 * PASSES)
        nc.vector.memset(wx_planes[:, first_planes, :].bitcast(I32), 0)
        nc.vector.memset(wx_planes[:, later_planes, :].bitcast(I32), 0)

        wx_codes = resident.tile([P, 3 * PASSES, FEATURES], U32, align_bytes=256)
        wx_words_by_partition = wx_words.rearrange("g p n t -> p g (n t)").bitcast(I32)

        def load_wx(gate, group):
            cols = slice(group * GROUP_COLS, (group + 1) * GROUP_COLS)
            both = slice(gate * PASSES, (gate + 1) * PASSES)
            nc.sync.dma_start(out=wx_codes[:, both, cols].bitcast(I32), in_=wx_words_by_partition[:, both, cols])

        wh_raw = {}

        def load_wh(gate, group, cs=range(PASSES)):
            cols = slice(group * GROUP_COLS, (group + 1) * GROUP_COLS)
            for c in cs:
                raw = raw_pool.tile([P, PACK, GROUP_COLS], BF16)
                rows = wh[gate, c * K_PASS : (c + 1) * K_PASS, cols]
                nc.sync.dma_start(out=raw[:], in_=rows.rearrange("(p t) n -> p t n", t=PACK))
                wh_raw[(gate, c, group)] = raw[:]

        load_rows(hid_rows, hid)
        load_rows(x_rows, x)
        load_wh(GATE_R, 0)
        load_planes(first_planes)
        load_wx(GATE_R, 0)
        load_wh(GATE_N, 0)
        load_planes(later_planes)
        load_wx(GATE_N, 0)
        load_wx(GATE_Z, 0)
        load_wh(GATE_Z, 0)
        for gate in (GATE_R, GATE_N, GATE_Z):
            load_wh(gate, 1)
            load_wx(gate, 1)

        identity = consts.tile([P, P], F32)
        make_identity(nc, identity[:])
        identity_bf16 = consts.tile([P, P], BF16)
        make_identity(nc, identity_bf16[:])

        def new_grouped(label):
            return [
                resident.tile([P, PASSES, BATCH * PACK // 2], BF16, align_bytes=256, name="%s_grouped_%d" % (label, side))
                for side in range(2)
            ]

        def flip_set(rows_tile, a):
            words = rows_tile[:].bitcast(F32)
            half = K_PASS // 2
            flipped = psum.tile([P, PASSES, 2, P], F32, name="flipped", tag="bank")
            for c in range(PASSES):
                for u in range(2):
                    nc.tensor.transpose(flipped[:, c, u, :], words[:, a, c * half + u : (c + 1) * half : 2], identity[:])
            return flipped

        def copy_set(flipped, grouped, a):
            side, i = divmod(a, 2)
            grouped_words = grouped[side][:].bitcast(F32).rearrange("p c (b u) -> p c b u", u=2)
            copy_out = nc.vector.tensor_copy if a % 2 == V_SETS else nc.scalar.copy
            copy_out(out=grouped_words[:, :, i * P : (i + 1) * P, :], in_=flipped[:].rearrange("p c u b -> p c b u"))

        def new_codes(label):
            codes = resident.tile([P, PASSES, BATCH], U32, align_bytes=256, name=label + "_codes")
            scales = resident.tile([P, PASSES, BATCH], U8, align_bytes=256, name=label + "_scales")
            return codes, scales

        def quantise_rows(grouped, codes, scales, side):
            cols = slice(side * BATCH // 2, (side + 1) * BATCH // 2)
            for c in range(PASSES):
                nc.vector.quantize_mx(
                    out=codes[:, c, cols].bitcast(FP8X4), scales=scales[:, c, cols],
                    in_=grouped[side][:, c, :],
                )

        wh_codes, wh_scales, wh_grouped = {}, {}, {}

        def regroup(gate, c, group):
            grouped = grouped_pool.tile([P, GROUP_COLS, PACK], BF16, align_bytes=256)
            src = wh_raw[(gate, c, group)].rearrange("p t (n i) -> p n t i", i=RUN)
            dst = grouped[:].rearrange("p (n i) t -> p n t i", i=RUN)
            runs = VECTOR_SHARE[(gate, group)]
            if runs > 0:
                nc.vector.tensor_copy(out=dst[:, :runs], in_=src[:, :runs])
            if runs < RUNS_ALL:
                nc.scalar.copy(out=dst[:, runs:], in_=src[:, runs:])
            wh_grouped[(gate, c, group)] = grouped

        def quantise(gate, c, group):
            codes = resident.tile([P, GROUP_COLS], U32, align_bytes=256, name="wh_codes_%d_%d_%d" % (gate, c, group))
            scales = resident.tile([P, GROUP_COLS], U8, align_bytes=256, name="wh_scales_%d_%d_%d" % (gate, c, group))
            nc.vector.quantize_mx(
                out=codes[:].bitcast(FP8X4), scales=scales[:],
                in_=wh_grouped[(gate, c, group)][:].rearrange("p n t -> p (n t)"),
            )
            wh_codes[(gate, c, group)] = codes
            wh_scales[(gate, c, group)] = scales

        def prepare(gate, group):
            for c in range(PASSES):
                regroup(gate, c, group)
            for c in range(PASSES):
                quantise(gate, c, group)

        def new_bank():
            return psum.tile([P, BATCH], F32, name="bank", tag="bank")

        def x_pass(bank, gate, j, c, start, stop):
            cols = slice(j * P, (j + 1) * P)
            g = gate * PASSES + c
            nc.tensor.matmul_mx(
                out=bank[:], lhsT=wx_codes[:, g, cols].bitcast(FP8X4), lhsT_scale=wx_planes[:, g, cols],
                rhs=x_codes[:, c, :].bitcast(FP8X4), rhs_scale=x_scales[:, c, :], start=start, stop=stop,
            )

        def hid_pass(bank, gate, j, c, start, stop):
            group, i = divmod(j, GROUP_TILES)
            cols = slice(i * P, (i + 1) * P)
            nc.tensor.matmul_mx(
                out=bank[:],
                lhsT=wh_codes[(gate, c, group)][:, cols].bitcast(FP8X4), lhsT_scale=wh_scales[(gate, c, group)][:, cols],
                rhs=hid_codes[:, c, :].bitcast(FP8X4), rhs_scale=hid_scales[:, c, :], start=start, stop=stop,
            )

        def tiles_of(group):
            return range(group * GROUP_TILES, (group + 1) * GROUP_TILES)

        r_value, y_value, n_value, z_value = {}, {}, {}, {}
        r_bank, nh_bank, nx_bank, z_bank, y_flipped, z_flipped = {}, {}, {}, {}, {}, {}

        def sigmoid_r(j):
            r_value[j] = gate_pool.tile([P, BATCH], F32, name="r_value", bufs=TILES)
            nc.scalar.activation(out=r_value[j][:], in_=r_bank[j][:], func=ACT.Sigmoid, bias=bias_r[:, j : j + 1], scale=1.0)

        def step_t(j):
            y_value[j] = gate_pool.tile([P, BATCH], F32, name="y_value")
            nc.vector.scalar_tensor_tensor(
                out=y_value[j][:], in0=nh_bank[j][:], scalar=bias_hn[:, j : j + 1], in1=r_value[j][:], op0=ALU.add, op1=ALU.mult,
            )

        def step_y(j):
            nc.vector.scalar_tensor_tensor(
                out=y_value[j][:], in0=nx_bank[j][:], scalar=bias_xn[:, j : j + 1], in1=y_value[j][:], op0=ALU.add, op1=ALU.add,
            )

        def flip(value, name):
            flipped = psum.tile([P, ROW_SETS, P], F32, name=name, tag="bank")
            for a in range(ROW_SETS):
                nc.tensor.transpose(flipped[:, a, :], value[:, a * P : (a + 1) * P], identity[:])
            return flipped

        def flip_y(j):
            y_flipped[j] = flip(y_value[j], "y_flipped")

        def flip_z(j):
            z_flipped[j] = flip(z_value[j], "z_flipped")

        def tanh_n(j):
            n_value[j] = gate_pool.tile([P, ROW_SETS, P], F32, name="n_value")
            nc.scalar.activation(out=n_value[j][:], in_=y_flipped[j][:], func=ACT.Tanh)

        def step_d(j):
            engine = nc.vector if j in (0,1,2,3,4,5,6) else nc.gpsimd
            engine.tensor_tensor(out=n_value[j][:], in0=n_value[j][:], in1=hid_rows[:, :, j * P : (j + 1) * P], op=ALU.subtract)

        def sigmoid_z(j):
            z_value[j] = gate_pool.tile([P, BATCH], F32, name="z_value", bufs=GROUP_TILES)
            nc.scalar.activation(out=z_value[j][:], in_=z_bank[j][:], func=ACT.Sigmoid, bias=minus_bias_z[:, j : j + 1], scale=-1.0)

        out_rows = out.rearrange("(p a) h -> p a h", a=ROW_SETS)
        results = {}

        def step_e(j):
            results[j] = result_pool.tile([P, ROW_SETS, P], F32, name="result")
            nc.vector.tensor_tensor(out=results[j][:], in0=z_flipped[j][:], in1=n_value[j][:], op=ALU.mult)

        def finish(j):
            cols = slice(j * P, (j + 1) * P)
            engine = nc.gpsimd if j in (0, 1, 2) else nc.vector
            engine.tensor_tensor(out=results[j][:], in0=results[j][:], in1=hid_rows[:, :, cols], op=ALU.add)
            nc.sync.dma_start(out=out_rows[:, :, cols], in_=results[j][:])

        def sigmoid_z_half(j, side):
            cols = slice(side * BATCH // 2, (side + 1) * BATCH // 2)
            nc.scalar.activation(out=z_value[j][:, cols], in_=z_bank[j][:, cols], func=ACT.Sigmoid, bias=minus_bias_z[:, j : j + 1], scale=-1.0)

        def flip_z_half(j, side):
            flipped = psum.tile([P, 2, P], F32, name="z_half", tag="bank")
            for i in range(2):
                a = 2 * side + i
                nc.tensor.transpose(flipped[:, i, :], z_value[j][:, a * P : (a + 1) * P], identity[:])
            z_flipped[(j, side)] = flipped

        def step_e_half(j, side):
            sets = slice(2 * side, 2 * side + 2)
            nc.vector.tensor_tensor(out=results[j][:, sets, :], in0=z_flipped[(j, side)][:], in1=n_value[j][:, sets, :], op=ALU.mult)

        def finish_half(j, side):
            sets = slice(2 * side, 2 * side + 2)
            cols = slice(j * P, (j + 1) * P)
            nc.vector.tensor_tensor(out=results[j][:, sets, :], in0=results[j][:, sets, :], in1=hid_rows[:, sets, cols], op=ALU.add)
            nc.sync.dma_start(out=out_rows[:, sets, cols], in_=results[j][:, sets, :])

        def x_half(banks, gate, group, start, stop):
            for j in tiles_of(group):
                if start:
                    banks[j] = new_bank()
                for c in range(PASSES):
                    x_pass(banks[j], gate, j, c, start and c == 0, stop and c == PASSES - 1)

        def hid_half(banks, gate, group, start, stop):
            for j in tiles_of(group):
                if start:
                    banks[j] = new_bank()
                for c in range(PASSES):
                    hid_pass(banks[j], gate, j, c, start and c == 0, stop and c == PASSES - 1)

        hid_grouped = new_grouped("hid")
        hid_codes, hid_scales = new_codes("hid")
        x_grouped = new_grouped("x")
        x_codes, x_scales = new_codes("x")
        hid_flipped = [flip_set(hid_rows, a) for a in range(ROW_SETS)]
        x_flipped = [flip_set(x_rows, a) for a in range(ROW_SETS)]
        bias_bank = psum.tile([P, P], BF16, tag="bank")
        nc.tensor.transpose(bias_bank[:], bias_rows[:], identity_bf16[:])
        idle_bank = psum.tile([P, BATCH], F32, tag="bank")
        for i in range(4):
            nc.tensor.matmul(idle_bank[:], lhsT=idle[:, 0:P], rhs=idle[:], start=True, stop=True)
        for a in range(3):
            copy_set(hid_flipped[a], hid_grouped, a)
        quantise_rows(hid_grouped, hid_codes, hid_scales, 0)
        copy_set(hid_flipped[3], hid_grouped, 3)
        quantise_rows(hid_grouped, hid_codes, hid_scales, 1)
        copy_set(x_flipped[0], x_grouped, 0)
        copy_set(x_flipped[1], x_grouped, 1)
        regroup(GATE_R, 0, 0)
        copy_set(x_flipped[2], x_grouped, 2)
        copy_set(x_flipped[3], x_grouped, 3)
        bias_cols = consts.tile([P, 64], F32)
        nc.vector.tensor_copy(out=bias_cols[:], in_=bias_bank[:, 0:64])

        quantise(GATE_R, 0, 0)
        quantise_rows(x_grouped, x_codes, x_scales, 0)
        def bias_of(first_row, gate):
            return bias_cols[:, first_row + gate * TILES : first_row + (gate + 1) * TILES]

        bias_r = consts.tile([P, TILES], F32)
        nc.vector.tensor_tensor(out=bias_r[:], in0=bias_of(0, GATE_R), in1=bias_of(32, GATE_R), op=ALU.add)
        minus_bias_z = consts.tile([P, TILES], F32)
        nc.vector.scalar_tensor_tensor(
            out=minus_bias_z[:], in0=bias_of(0, GATE_Z), scalar=-1.0, in1=bias_of(32, GATE_Z), op0=ALU.mult, op1=ALU.subtract,
        )
        bias_xn = bias_of(0, GATE_N)
        bias_hn = bias_of(32, GATE_N)

        regroup(GATE_R, 1, 0)
        quantise_rows(x_grouped, x_codes, x_scales, 1)
        quantise(GATE_R, 1, 0)
        for j in tiles_of(0):
            r_bank[j] = new_bank()
        for j in tiles_of(0):
            hid_pass(r_bank[j], GATE_R, j, 0, True, False)
        for c in range(PASSES):
            for j in tiles_of(0):
                x_pass(r_bank[j], GATE_R, j, c, False, False)
        for j in tiles_of(0):
            hid_pass(r_bank[j], GATE_R, j, 1, False, True)
        for group in range(GROUPS):
            if group > 0:
                x_half(r_bank, GATE_R, group, True, False)
                for j in tiles_of(group - 1):
                    flip_z(j)
            prepare(GATE_N, group)
            if group > 0:
                hid_half(r_bank, GATE_R, group, False, True)
            for j in tiles_of(group):
                sigmoid_r(j)
            if group > 0:
                for j in tiles_of(group - 1):
                    step_e(j)
                    if j in EARLY_ADDS:
                        finish(j)
            hid_half(nh_bank, GATE_N, group, True, True)
            for j in tiles_of(group):
                step_t(j)
            x_half(nx_bank, GATE_N, group, True, True)
            if group == GROUPS - 1:
                prepare(GATE_Z, group)
            for j in tiles_of(group):
                step_y(j)
            if group < GROUPS - 1:
                prepare(GATE_Z, group)
            if group == GROUPS - 1:
                for j in tiles_of(group - 1):
                    if j not in EARLY_ADDS:
                        finish(j)
                break
            prepare(GATE_R, group + 1)
            x_half(z_bank, GATE_Z, group, True, False)
            for j in tiles_of(group):
                flip_y(j)
            for j in tiles_of(group):
                tanh_n(j)
                step_d(j)
            hid_half(z_bank, GATE_Z, group, False, True)
            for j in tiles_of(group):
                sigmoid_z(j)
        first, second, third, fourth = tiles_of(GROUPS - 1)

        def all_passes(j):
            z_bank[j] = new_bank()
            for c in range(PASSES):
                x_pass(z_bank[j], GATE_Z, j, c, c == 0, False)
            for c in range(PASSES):
                hid_pass(z_bank[j], GATE_Z, j, c, False, c == PASSES - 1)

        all_passes(first)
        sigmoid_z(first)
        all_passes(second)
        sigmoid_z(second)
        for j in tiles_of(GROUPS - 1):
            flip_y(j)
            tanh_n(j)
        flip_z(first)
        flip_z(second)
        all_passes(third)
        sigmoid_z(third)
        all_passes(fourth)
        z_value[fourth] = gate_pool.tile([P, BATCH], F32, name="z_value", bufs=GROUP_TILES)
        results[fourth] = result_pool.tile([P, ROW_SETS, P], F32, name="result")
        flip_z(third)
        for side in range(2):
            sigmoid_z_half(fourth, side)
            flip_z_half(fourth, side)
        step_d(first)
        step_d(second)
        step_d(third)
        step_d(fourth)
        step_e(first)
        step_e(second)
        finish(first)
        finish(second)
        step_e(third)
        step_e_half(fourth, 0)
        finish(third)
        step_e_half(fourth, 1)
        finish_half(fourth, 0)
        finish_half(fourth, 1)
